import numpy as np
import ml_dtypes


def mxq(x, axis, fmt="e4m3"):
    dtype, down = {"e4m3": (ml_dtypes.float8_e4m3fn, 7), "e5m2": (ml_dtypes.float8_e5m2, 14)}[fmt]
    v = np.moveaxis(np.asarray(x, np.float32).astype(ml_dtypes.bfloat16).astype(np.float64), axis, -1)
    blocks = v.reshape(v.shape[:-1] + (-1, 32))
    amax = np.abs(blocks).max(-1, keepdims=True)
    byte = np.maximum(np.where(amax > 0, np.frexp(amax)[1] - 1 + 127, 0) - down, 1)
    scale = np.exp2(byte - 127.0)
    codes = (blocks / scale).astype(np.float32).astype(dtype).astype(np.float64)
    return np.moveaxis((codes * scale).reshape(v.shape), -1, axis)


WIDE = False


def mx_kscale(k):
    if not WIDE:
        return np.ones(k)
    levels = np.array([10, -10, 5, -5, 0])
    if k % 512:
        return np.exp2(np.random.permutation(np.resize(levels, k // 32))).repeat(32)
    a = np.empty((k // 512, 16))
    for p in range(k // 512):
        a[p, :8] = np.random.permutation(np.resize(levels, 8))
        for g in range(8):
            far = levels[np.abs(levels - a[p, g]) >= 10]
            a[p, g + 8] = far[np.random.randint(len(far))]
    return np.exp2(a.ravel()).repeat(32)


BF16 = ml_dtypes.bfloat16


def bf(x):
    return np.asarray(x, np.float32).astype(BF16)


def f64(x):
    return np.asarray(x).astype(np.float64)


B, S, HID, NH, NOPE, ROPE, VD, KV_RANK, SW, QB = 1, 2048, 1024, 8, 64, 128, 128, 512, 384, 128


def rotate_half(x):
    h = x.shape[-1] // 2
    return np.concatenate([-x[..., h:], x[..., :h]], axis=-1)


def rope_tables():
    pos = np.arange(S, dtype=np.float64)
    inv = 1.0 / (10000.0 ** (np.arange(0, ROPE, 2, dtype=np.float64) / ROPE))
    ang = pos[:, None] * inv[None, :]
    ang = np.concatenate([ang, ang], axis=-1)
    return bf(np.broadcast_to(np.cos(ang)[None], (B, S, ROPE))), bf(np.broadcast_to(np.sin(ang)[None], (B, S, ROPE)))


def setup_inputs():
    s, t = mx_kscale(HID), mx_kscale(KV_RANK)
    col = np.concatenate([t, np.ones(ROPE)])
    cos, sin = rope_tables()
    return {"hidden_states": bf(np.random.standard_normal((B, S, HID)) * s), "cos": cos, "sin": sin,
            "Wkva": bf(np.random.standard_normal((HID, KV_RANK + ROPE)) / np.sqrt(HID) / s[:, None] * col),
            "bkva": bf(np.random.standard_normal(KV_RANK + ROPE) * 0.1 * col),
            "Wkvb": bf(np.random.standard_normal((KV_RANK, NH * (NOPE + VD))) / np.sqrt(KV_RANK) / t[:, None])}


def reference(hidden_states, cos, sin, Wkva, bkva, Wkvb):
    ckv = (mxq(f64(hidden_states), 2, "e4m3") @ mxq(f64(Wkva), 0, "e4m3")) + f64(bkva)
    kv_lat, k_rope = ckv[..., :KV_RANK], ckv[..., KV_RANK:]
    kv = (mxq(kv_lat, 2, "e4m3") @ mxq(f64(Wkvb), 0, "e4m3")).reshape(B, S, NH, NOPE + VD).transpose(0, 2, 1, 3)
    k_nope, v = kv[..., :NOPE], kv[..., NOPE:]
    k_rope = k_rope.reshape(B, 1, S, ROPE)
    c, si = f64(cos)[:, None], f64(sin)[:, None]
    k_rope = k_rope * c + rotate_half(k_rope) * si
    k_rope = np.broadcast_to(k_rope, (B, NH, S, ROPE))
    kk = np.concatenate([k_nope, k_rope], axis=-1)
    return kk, np.ascontiguousarray(v)

@@ -1,0 +1,315 @@
+from contextlib import ExitStack
+
+import concourse.mybir as mybir
+from concourse.masks import make_identity
+
+F32 = mybir.dt.float32
+BF16 = mybir.dt.bfloat16
+U32 = mybir.dt.uint32
+U8 = mybir.dt.uint8
+FP8X4 = mybir.dt.float8_e4m3fn_x4
+ADD = mybir.AluOpType.add
+MULT = mybir.AluOpType.mult
+
+P = 128
+PACK = 4
+K_PASS = P * PACK
+
+SEQ = 2048
+HID = 1024
+HEADS = 8
+NOPE = 64
+ROPE = 128
+VDIM = 128
+RANK = 512
+
+HID_PASSES = HID // K_PASS
+WORD_BLOCKS = HID // 2 // P
+J = 4
+GROUPS = SEQ // (P * J)
+TILES = GROUPS * J
+HALF_HEADS = HEADS // 2
+HALF_ROPE = ROPE // 2
+KV_CHUNK = 512
+KV_CHUNKS = HEADS * (NOPE + VDIM) // KV_CHUNK
+
+GROUP_LAG = J
+
+FLOPS = 2 * SEQ * HID * (RANK + ROPE) + 2 * SEQ * RANK * HEADS * (NOPE + VDIM)
+
+
+def tile_gptossmlaattention_pa_kernel(tc, hidden_states, cos, sin, Wkva, bkva, Wkvb, out_0, out_1):
+    nc = tc.nc
+
+    hid_dram = hidden_states[0, :, :].rearrange("(p i) k -> p (i k)", p=P)
+    cos_dram = cos[0, :, :].rearrange("(p s) d -> p (s d)", p=P)
+    sin_dram = sin[0, :, :].rearrange("(p s) d -> p (s d)", p=P)
+    kk_dram = out_0[0, :, :, :].rearrange("h (p g j) d -> g p h (j d)", p=P, j=J)
+    v_dram = out_1[0, :, :, :].rearrange("h (p g j) d -> g p h (j d)", p=P, j=J)
+    wa_dram = Wkva.rearrange("(kp p t) c -> kp p t c", kp=HID_PASSES, p=P, t=PACK)
+    wb_dram = Wkvb.rearrange("(p t) n -> p t n", t=PACK)
+
+    with ExitStack() as ctx:
+        const = ctx.enter_context(tc.tile_pool(name="const", bufs=1))
+        inputs = ctx.enter_context(tc.tile_pool(name="inputs", bufs=1))
+        wstage = ctx.enter_context(tc.tile_pool(name="wstage", bufs=2))
+        work = ctx.enter_context(tc.tile_pool(name="work", bufs=3))
+        rope_pool = ctx.enter_context(tc.tile_pool(name="rope", bufs=2))
+        kk_pool = ctx.enter_context(tc.tile_pool(name="kk", bufs=2))
+        v_pool = ctx.enter_context(tc.tile_pool(name="v", bufs=6))
+        psum_xt = ctx.enter_context(tc.psum_pool(name="psum_xt", bufs=2))
+        psum_lat = ctx.enter_context(tc.psum_pool(name="psum_lat", bufs=2))
+        psum_rope = ctx.enter_context(tc.psum_pool(name="psum_rope", bufs=1))
+        psum_kv = ctx.enter_context(tc.psum_pool(name="psum_kv", bufs=3))
+
+        lat_bias = const.tile([P, PACK], BF16)
+        nc.scalar.dma_start(out=lat_bias[:], in_=bkva[0:RANK].rearrange("(p t) -> p t", t=PACK))
+        bias_row = const.tile([P, ROPE], BF16)
+        nc.vector.memset(bias_row[:], 0.0)
+        nc.scalar.dma_start(out=bias_row[0:1, :], in_=bkva[RANK : RANK + ROPE].rearrange("(r c) -> r c", r=1))
+
+        raw_a = inputs.tile([P, HID_PASSES, PACK, RANK + ROPE], BF16)
+        for kp in range(HID_PASSES):
+            nc.sync.dma_start(out=raw_a[:, kp, :, :], in_=wa_dram[kp])
+        hid_rows = {}
+
+        def load_hidden(first, count):
+            raw = inputs.tile([P, count * HID], BF16, name="hid_raw%d" % first)
+            nc.sync.dma_start(out=raw[:], in_=hid_dram[:, first * HID : (first + count) * HID])
+            for k in range(count):
+                hid_rows[first + k] = raw[:, k * HID : (k + 1) * HID]
+
+        load_hidden(0, J // 2)
+        load_hidden(J // 2, J // 2)
+        raw_b = inputs.tile([P, PACK, HEADS * (NOPE + VDIM)], BF16)
+        half_cols = HALF_HEADS * (NOPE + VDIM)
+        for half in range(2):
+            cols = slice(half * half_cols, (half + 1) * half_cols)
+            nc.sync.dma_start(out=raw_b[:, :, cols], in_=wb_dram[:, :, cols])
+        load_hidden(J, J)
+        cos_sb = inputs.tile([P, GROUPS, J, ROPE], BF16)
+        sin_sb = inputs.tile([P, GROUPS, J, ROPE], BF16)
+        nc.sync.dma_start(out=cos_sb[:].rearrange("p g j d -> p (g j d)"), in_=cos_dram)
+        nc.sync.dma_start(out=sin_sb[:].rearrange("p g j d -> p (g j d)"), in_=sin_dram)
+        for g in range(2, GROUPS):
+            load_hidden(g * J, J)
+
+        ident_f32 = const.tile([P, P], F32)
+        make_identity(nc, ident_f32[:])
+        ones = const.tile([P, P], BF16)
+        nc.vector.memset(ones[:], 1.0)
+        rope_bias = const.tile([P, ROPE], F32)
+
+        def spread_biases():
+            rope_bias_ps = psum_xt.tile([P, ROPE], F32, tag="xt")
+            nc.tensor.matmul(out=rope_bias_ps[:], lhsT=ones[:], rhs=bias_row[:], start=True, stop=True)
+            nc.vector.tensor_copy(out=rope_bias[:], in_=rope_bias_ps[:])
+
+        a_codes = const.tile([P, HID_PASSES, RANK + ROPE], U32, align_bytes=64)
+        a_scales = const.tile([P, HID_PASSES, RANK + ROPE], U8, align_bytes=64)
+        grouped_a = []
+        for kp in range(HID_PASSES):
+            grouped = wstage.tile([P, RANK + ROPE, PACK], BF16, align_bytes=64, name="grouped_a", tag="grouped_a")
+            nc.vector.tensor_copy(
+                out=grouped[:, 0:RANK, :].rearrange("p (b m) t -> p b m t", b=PACK),
+                in_=raw_a[:, kp, :, 0:RANK].rearrange("p t (m b) -> p b m t", b=PACK),
+            )
+            nc.vector.tensor_copy(
+                out=grouped[:, RANK:, :].rearrange("p (c i) t -> p c t i", i=4),
+                in_=raw_a[:, kp, :, RANK:].rearrange("p t (c i) -> p c t i", i=4),
+            )
+            grouped_a.append(grouped)
+        for kp in range(HID_PASSES):
+            for cols in (slice(0, RANK), slice(RANK, RANK + ROPE)):
+                nc.vector.quantize_mx(
+                    out=a_codes[:, kp, cols].bitcast(FP8X4),
+                    scales=a_scales[:, kp, cols],
+                    in_=grouped_a[kp][:, cols, :].rearrange("p c t -> p (c t)"),
+                )
+
+        b_codes = const.tile([P, KV_CHUNKS * KV_CHUNK], U32, align_bytes=64)
+        b_scales = const.tile([P, KV_CHUNKS * KV_CHUNK], U8, align_bytes=64)
+        raw_b_heads = raw_b[:].rearrange("p t (h x) -> p t h x", x=NOPE + VDIM)
+        b_sources = [
+            raw_b_heads[:, :, 0:HALF_HEADS, NOPE:],
+            raw_b_heads[:, :, HALF_HEADS:HEADS, NOPE:],
+            raw_b_heads[:, :, :, 0:NOPE],
+        ]
+        grouped_b = {}
+
+        def regroup_b(n):
+            grouped_b[n] = wstage.tile([P, KV_CHUNK, PACK], BF16, align_bytes=64, name="grouped_b", tag="grouped_b")
+            copy = nc.scalar.copy if n < 2 else nc.vector.tensor_copy
+            copy(
+                out=grouped_b[n][:].rearrange("p (h d) t -> p h d t", h=b_sources[n].shape[2]),
+                in_=b_sources[n].rearrange("p t h d -> p h d t"),
+            )
+
+        def quantise_b(n):
+            cols = slice(n * KV_CHUNK, (n + 1) * KV_CHUNK)
+            nc.vector.quantize_mx(
+                out=b_codes[:, cols].bitcast(FP8X4),
+                scales=b_scales[:, cols],
+                in_=grouped_b[n][:].rearrange("p c t -> p (c t)"),
+            )
+
+        hid_q = {}
+        lat_q = {}
+        rope_ps = {}
+        rope_sb = {}
+        kk_stage = {}
+        v_stage = {}
+
+        def front(i):
+            hid_words = hid_rows[i].bitcast(F32)
+            xt = psum_xt.tile([P, WORD_BLOCKS, P], F32, tag="xt")
+            for q in range(WORD_BLOCKS):
+                kp, u = divmod(q, 2)
+                nc.tensor.transpose(
+                    out=xt[:, q, :], in_=hid_words[:, 2 * P * kp + u : 2 * P * (kp + 1) : 2], identity=ident_f32[:]
+                )
+            hid_grouped = work.tile([P, HID_PASSES * P * PACK], BF16, align_bytes=64)
+            nc.scalar.copy(
+                out=hid_grouped[:].bitcast(F32).rearrange("p (kp c u) -> p kp c u", kp=HID_PASSES, u=2),
+                in_=xt[:].rearrange("p (kp u) c -> p kp c u", u=2),
+            )
+            hid_codes = work.tile([P, HID_PASSES, P], U32, align_bytes=64)
+            hid_scales = work.tile([P, HID_PASSES, P], U8, align_bytes=64)
+            nc.vector.quantize_mx(
+                out=hid_codes[:].rearrange("p kp c -> p (kp c)").bitcast(FP8X4),
+                scales=hid_scales[:].rearrange("p kp c -> p (kp c)"),
+                in_=hid_grouped[:],
+            )
+            hid_q[i] = (hid_codes, hid_scales)
+
+        def middle(i):
+            g, j = divmod(i, J)
+            hid_codes, hid_scales = hid_q[i]
+            if j == 0:
+                rope_ps[g] = psum_rope.tile([P, J, ROPE], F32, name="rope_ps")
+                lat_q[g] = (
+                    work.tile([P, J, P], U32, align_bytes=64, name="lat_codes"),
+                    work.tile([P, J, P], U8, align_bytes=64, name="lat_scales"),
+                )
+            lat_ps = psum_lat.tile([P, PACK, P], F32)
+            for t in range(PACK):
+                for kp in range(HID_PASSES):
+                    nc.tensor.matmul_mx(
+                        out=lat_ps[:, t, :],
+                        lhsT=a_codes[:, kp, t * P : (t + 1) * P].bitcast(FP8X4),
+                        lhsT_scale=a_scales[:, kp, t * P : (t + 1) * P],
+                        rhs=hid_codes[:, kp, :].bitcast(FP8X4),
+                        rhs_scale=hid_scales[:, kp, :],
+                        start=(kp == 0),
+                        stop=(kp == HID_PASSES - 1),
+                    )
+            for kp in range(HID_PASSES):
+                nc.tensor.matmul_mx(
+                    out=rope_ps[g][:, j, :],
+                    lhsT=hid_codes[:, kp, :].bitcast(FP8X4),
+                    lhsT_scale=hid_scales[:, kp, :],
+                    rhs=a_codes[:, kp, RANK : RANK + ROPE].bitcast(FP8X4),
+                    rhs_scale=a_scales[:, kp, RANK : RANK + ROPE],
+                    start=(kp == 0),
+                    stop=(kp == HID_PASSES - 1),
+                )
+            lat_grouped = work.tile([P, P, PACK], BF16, align_bytes=64)
+            nc.vector.tensor_tensor(
+                out=lat_grouped[:],
+                in0=lat_ps[:].rearrange("p t c -> p c t"),
+                in1=lat_bias[:].unsqueeze(1).to_broadcast([P, P, PACK]),
+                op=ADD,
+            )
+            lat_codes, lat_scales = lat_q[g]
+            nc.vector.quantize_mx(
+                out=lat_codes[:, j, :].bitcast(FP8X4),
+                scales=lat_scales[:, j, :],
+                in_=lat_grouped[:].rearrange("p c t -> p (c t)"),
+            )
+
+        def rotate(g, part):
+            if part == 0:
+                kk_stage[g] = kk_pool.tile([P, HEADS, J, NOPE + ROPE], F32, name="kk_stage")
+                rope_sb[g] = (
+                    rope_pool.tile([P, J, ROPE], F32, name="k_rope"),
+                    rope_pool.tile([P, J, ROPE], F32, name="k_rot"),
+                    rope_pool.tile([P, J, ROPE], F32, name="crossed"),
+                )
+            k_rope, k_rot, crossed = rope_sb[g]
+            lo = slice(0, HALF_ROPE)
+            hi = slice(HALF_ROPE, ROPE)
+            if part == 0:
+                nc.vector.tensor_tensor(
+                    out=k_rope[:],
+                    in0=rope_ps[g][:],
+                    in1=rope_bias[:].unsqueeze(1).to_broadcast([P, J, ROPE]),
+                    op=ADD,
+                )
+            if part == 1:
+                nc.vector.tensor_tensor(out=k_rot[:], in0=k_rope[:], in1=cos_sb[:, g, :, :], op=MULT)
+                nc.vector.scalar_tensor_tensor(
+                    out=crossed[:, :, lo], in0=k_rope[:, :, hi], scalar=-1.0, in1=sin_sb[:, g, :, lo], op0=MULT, op1=MULT
+                )
+                nc.vector.tensor_tensor(out=crossed[:, :, hi], in0=k_rope[:, :, lo], in1=sin_sb[:, g, :, hi], op=MULT)
+            if part == 2:
+                nc.vector.tensor_tensor(out=k_rot[:], in0=k_rot[:], in1=crossed[:], op=ADD)
+            if part >= 2:
+                heads = slice((part - 2) * HALF_HEADS, (part - 1) * HALF_HEADS)
+                nc.vector.tensor_copy(
+                    out=kk_stage[g][:, heads, :, NOPE:],
+                    in_=k_rot[:].unsqueeze(1).to_broadcast([P, HALF_HEADS, J, ROPE]),
+                )
+
+        def second(g, n, j):
+            if n == 0 and j == 0:
+                v_stage[g] = [
+                    v_pool.tile([P, HALF_HEADS, J, VDIM], F32, name="v_stage", tag="v_stage") for half in range(2)
+                ]
+            lat_codes, lat_scales = lat_q[g]
+            kv_ps = psum_kv.tile([P, KV_CHUNK], F32)
+            cols = slice(n * KV_CHUNK, (n + 1) * KV_CHUNK)
+            nc.tensor.matmul_mx(
+                out=kv_ps[:],
+                lhsT=lat_codes[:, j, :].bitcast(FP8X4),
+                lhsT_scale=lat_scales[:, j, :],
+                rhs=b_codes[:, cols].bitcast(FP8X4),
+                rhs_scale=b_scales[:, cols],
+                start=True,
+                stop=True,
+            )
+            if n < 2:
+                nc.scalar.copy(out=v_stage[g][n][:, :, j, :], in_=kv_ps[:].rearrange("p (h d) -> p h d", d=VDIM))
+                if j == J - 1:
+                    heads = slice(n * HALF_HEADS, (n + 1) * HALF_HEADS)
+                    nc.sync.dma_start(
+                        out=v_dram[g, :, heads, :], in_=v_stage[g][n][:].rearrange("p h j d -> p h (j d)")
+                    )
+            else:
+                nc.scalar.copy(out=kk_stage[g][:, :, j, 0:NOPE], in_=kv_ps[:].rearrange("p (h d) -> p h d", d=NOPE))
+
+        def store_kk(g):
+            for half in range(2):
+                heads = slice(half * HALF_HEADS, (half + 1) * HALF_HEADS)
+                nc.sync.dma_start(
+                    out=kk_dram[g, :, heads, :], in_=kk_stage[g][:, heads, :, :].rearrange("p h j d -> p h (j d)")
+                )
+
+        for s in range(TILES + GROUP_LAG):
+            if s % 2 == 0 and 1 <= s // 2 <= KV_CHUNKS:
+                quantise_b(s // 2 - 1)
+            if s >= GROUP_LAG:
+                g, quarter = divmod(s - GROUP_LAG, J)
+                for unit in range(KV_CHUNKS * quarter, KV_CHUNKS * (quarter + 1)):
+                    second(g, *divmod(unit, J))
+            if s < TILES:
+                front(s)
+            if s % 2 == 1 and s // 2 < KV_CHUNKS:
+                regroup_b(s // 2)
+            if s == 1:
+                spread_biases()
+            if 1 <= s <= TILES:
+                middle(s - 1)
+            if s >= GROUP_LAG:
+                rotate(g, quarter)
+                if quarter == J - 1:
+                    store_kk(g)

@@ -33,6 +33,8 @@ HALF_ROPE = ROPE // 2
 KV_CHUNK = 512
 KV_CHUNKS = HEADS * (NOPE + VDIM) // KV_CHUNK
 
+V_GROUPS = ((0,), (1,), (2, 3))
+
 GROUP_LAG = J
 
 FLOPS = 2 * SEQ * HID * (RANK + ROPE) + 2 * SEQ * RANK * HEADS * (NOPE + VDIM)
@@ -45,18 +47,18 @@ def tile_gptossmlaattention_pa_kernel(tc, hidden_states, cos, sin, Wkva, bkva, W
     cos_dram = cos[0, :, :].rearrange("(p s) d -> p (s d)", p=P)
     sin_dram = sin[0, :, :].rearrange("(p s) d -> p (s d)", p=P)
     kk_dram = out_0[0, :, :, :].rearrange("h (p g j) d -> g p h (j d)", p=P, j=J)
-    v_dram = out_1[0, :, :, :].rearrange("h (p g j) d -> g p h (j d)", p=P, j=J)
+    v_dram = out_1[0, :, :, :].rearrange("h (p s) d -> p h (s d)", p=P)
     wa_dram = Wkva.rearrange("(kp p t) c -> kp p t c", kp=HID_PASSES, p=P, t=PACK)
     wb_dram = Wkvb.rearrange("(p t) n -> p t n", t=PACK)
 
     with ExitStack() as ctx:
         const = ctx.enter_context(tc.tile_pool(name="const", bufs=1))
         inputs = ctx.enter_context(tc.tile_pool(name="inputs", bufs=1))
-        wstage = ctx.enter_context(tc.tile_pool(name="wstage", bufs=2))
+        wstage = ctx.enter_context(tc.tile_pool(name="wstage", bufs=3))
         work = ctx.enter_context(tc.tile_pool(name="work", bufs=3))
         rope_pool = ctx.enter_context(tc.tile_pool(name="rope", bufs=2))
         kk_pool = ctx.enter_context(tc.tile_pool(name="kk", bufs=2))
-        v_pool = ctx.enter_context(tc.tile_pool(name="v", bufs=6))
+        v_pool = ctx.enter_context(tc.tile_pool(name="v", bufs=1))
         psum_xt = ctx.enter_context(tc.psum_pool(name="psum_xt", bufs=2))
         psum_lat = ctx.enter_context(tc.psum_pool(name="psum_lat", bufs=2))
         psum_rope = ctx.enter_context(tc.psum_pool(name="psum_rope", bufs=1))
@@ -109,7 +111,7 @@ def tile_gptossmlaattention_pa_kernel(tc, hidden_states, cos, sin, Wkva, bkva, W
         a_scales = const.tile([P, HID_PASSES, RANK + ROPE], U8, align_bytes=64)
         grouped_a = []
         for kp in range(HID_PASSES):
-            grouped = wstage.tile([P, RANK + ROPE, PACK], BF16, align_bytes=64, name="grouped_a", tag="grouped_a")
+            grouped = wstage.tile([P, RANK + ROPE, PACK], BF16, align_bytes=64, name="grouped_a", tag="grouped")
             nc.vector.tensor_copy(
                 out=grouped[:, 0:RANK, :].rearrange("p (b m) t -> p b m t", b=PACK),
                 in_=raw_a[:, kp, :, 0:RANK].rearrange("p t (m b) -> p b m t", b=PACK),
@@ -138,7 +140,7 @@ def tile_gptossmlaattention_pa_kernel(tc, hidden_states, cos, sin, Wkva, bkva, W
         grouped_b = {}
 
         def regroup_b(n):
-            grouped_b[n] = wstage.tile([P, KV_CHUNK, PACK], BF16, align_bytes=64, name="grouped_b", tag="grouped_b")
+            grouped_b[n] = wstage.tile([P, KV_CHUNK, PACK], BF16, align_bytes=64, name="grouped_b", tag="grouped")
             copy = nc.scalar.copy if n < 2 else nc.vector.tensor_copy
             copy(
                 out=grouped_b[n][:].rearrange("p (h d) t -> p h d t", h=b_sources[n].shape[2]),
@@ -261,9 +263,11 @@ def tile_gptossmlaattention_pa_kernel(tc, hidden_states, cos, sin, Wkva, bkva, W
                 )
 
         def second(g, n, j):
-            if n == 0 and j == 0:
+            together = [groups for groups in V_GROUPS if g in groups][0]
+            if n == 0 and j == 0 and g == together[0]:
+                tokens = len(together) * J
                 v_stage[g] = [
-                    v_pool.tile([P, HALF_HEADS, J, VDIM], F32, name="v_stage", tag="v_stage") for half in range(2)
+                    v_pool.tile([P, HALF_HEADS, tokens, VDIM], F32, name="v_stage_%d_%d" % (g, half)) for half in range(2)
                 ]
             lat_codes, lat_scales = lat_q[g]
             kv_ps = psum_kv.tile([P, KV_CHUNK], F32)
@@ -278,12 +282,14 @@ def tile_gptossmlaattention_pa_kernel(tc, hidden_states, cos, sin, Wkva, bkva, W
                 stop=True,
             )
             if n < 2:
-                nc.scalar.copy(out=v_stage[g][n][:, :, j, :], in_=kv_ps[:].rearrange("p (h d) -> p h d", d=VDIM))
-                if j == J - 1:
+                stage = v_stage[together[0]][n]
+                nc.scalar.copy(
+                    out=stage[:, :, (g - together[0]) * J + j, :], in_=kv_ps[:].rearrange("p (h d) -> p h d", d=VDIM)
+                )
+                if j == J - 1 and g == together[-1]:
                     heads = slice(n * HALF_HEADS, (n + 1) * HALF_HEADS)
-                    nc.sync.dma_start(
-                        out=v_dram[g, :, heads, :], in_=v_stage[g][n][:].rearrange("p h j d -> p h (j d)")
-                    )
+                    run = slice(together[0] * J * VDIM, (together[-1] + 1) * J * VDIM)
+                    nc.sync.dma_start(out=v_dram[:, heads, run], in_=stage[:].rearrange("p h j d -> p h (j d)"))
             else:
                 nc.scalar.copy(out=kk_stage[g][:, :, j, 0:NOPE], in_=kv_ps[:].rearrange("p (h d) -> p h d", d=NOPE))
 

@@ -22,20 +22,19 @@ NOPE = 64
 ROPE = 128
 VDIM = 128
 RANK = 512
+KDIM = NOPE + ROPE
 
 HID_PASSES = HID // K_PASS
-WORD_BLOCKS = HID // 2 // P
-J = 4
-GROUPS = SEQ // (P * J)
-TILES = GROUPS * J
+TILES = SEQ // P
+PAIR = 2
+PAIRS = TILES // PAIR
 HALF_HEADS = HEADS // 2
 HALF_ROPE = ROPE // 2
 KV_CHUNK = 512
-KV_CHUNKS = HEADS * (NOPE + VDIM) // KV_CHUNK
+K_CHUNK = 2
 
-V_GROUPS = ((0,), (1,), (2, 3))
-
-GROUP_LAG = J
+K_RUNS = ((0, 4), (4, 8), (8, 12), (12, 16))
+V_RUNS = ((0, 4), (4, 8), (8, 16))
 
 FLOPS = 2 * SEQ * HID * (RANK + ROPE) + 2 * SEQ * RANK * HEADS * (NOPE + VDIM)
 
@@ -46,55 +45,66 @@ def tile_gptossmlaattention_pa_kernel(tc, hidden_states, cos, sin, Wkva, bkva, W
     hid_dram = hidden_states[0, :, :].rearrange("(p i) k -> p (i k)", p=P)
     cos_dram = cos[0, :, :].rearrange("(p s) d -> p (s d)", p=P)
     sin_dram = sin[0, :, :].rearrange("(p s) d -> p (s d)", p=P)
-    kk_dram = out_0[0, :, :, :].rearrange("h (p g j) d -> g p h (j d)", p=P, j=J)
+    kk_dram = out_0[0, :, :, :].rearrange("h (p s) d -> p h (s d)", p=P)
     v_dram = out_1[0, :, :, :].rearrange("h (p s) d -> p h (s d)", p=P)
-    wa_dram = Wkva.rearrange("(kp p t) c -> kp p t c", kp=HID_PASSES, p=P, t=PACK)
-    wb_dram = Wkvb.rearrange("(p t) n -> p t n", t=PACK)
+    wa_dram = Wkva.rearrange("(kp p t) c -> kp p (t c)", kp=HID_PASSES, p=P, t=PACK)
+    wb_dram = Wkvb.rearrange("(p t) n -> p (t n)", t=PACK)
 
     with ExitStack() as ctx:
         const = ctx.enter_context(tc.tile_pool(name="const", bufs=1))
-        inputs = ctx.enter_context(tc.tile_pool(name="inputs", bufs=1))
+        big = ctx.enter_context(tc.tile_pool(name="big", bufs=1))
         wstage = ctx.enter_context(tc.tile_pool(name="wstage", bufs=3))
         work = ctx.enter_context(tc.tile_pool(name="work", bufs=3))
         rope_pool = ctx.enter_context(tc.tile_pool(name="rope", bufs=2))
-        kk_pool = ctx.enter_context(tc.tile_pool(name="kk", bufs=2))
-        v_pool = ctx.enter_context(tc.tile_pool(name="v", bufs=1))
         psum_xt = ctx.enter_context(tc.psum_pool(name="psum_xt", bufs=2))
         psum_lat = ctx.enter_context(tc.psum_pool(name="psum_lat", bufs=2))
         psum_rope = ctx.enter_context(tc.psum_pool(name="psum_rope", bufs=1))
         psum_kv = ctx.enter_context(tc.psum_pool(name="psum_kv", bufs=3))
 
-        lat_bias = const.tile([P, PACK], BF16)
-        nc.scalar.dma_start(out=lat_bias[:], in_=bkva[0:RANK].rearrange("(p t) -> p t", t=PACK))
+        KK_TILE = HEADS * KDIM * 4
+        V_TILE = HALF_HEADS * VDIM * 4
+        raw_a_at = 0
+        raw_b_at = raw_a_at + HID_PASSES * PACK * (RANK + ROPE) * 2
+        hid_at = raw_b_at + PACK * HEADS * (NOPE + VDIM) * 2
+        at = hid_at + TILES * HID * 2
+        kk_at = {}
+        for k, (first, end) in enumerate(K_RUNS):
+            kk_at[first] = at + k % 3 * 4 * KK_TILE
+        at += 12 * KK_TILE
+        v_at = {(8, 0): raw_a_at, (8, 1): hid_at}
+        for first in (0, 4):
+            for half in range(2):
+                v_at[(first, half)] = at
+                at += 4 * V_TILE
+
         bias_row = const.tile([P, ROPE], BF16)
         nc.vector.memset(bias_row[:], 0.0)
-        nc.scalar.dma_start(out=bias_row[0:1, :], in_=bkva[RANK : RANK + ROPE].rearrange("(r c) -> r c", r=1))
-
-        raw_a = inputs.tile([P, HID_PASSES, PACK, RANK + ROPE], BF16)
+        raw_a = big.tile([P, HID_PASSES, PACK, RANK + ROPE], BF16, offset=raw_a_at)
         for kp in range(HID_PASSES):
-            nc.sync.dma_start(out=raw_a[:, kp, :, :], in_=wa_dram[kp])
+            nc.sync.dma_start(out=raw_a[:, kp, :, :].rearrange("p t c -> p (t c)"), in_=wa_dram[kp])
+        lat_bias = const.tile([P, PACK], BF16)
+        nc.sync.dma_start(out=lat_bias[:], in_=bkva[0:RANK].rearrange("(p t) -> p t", t=PACK))
+        nc.sync.dma_start(out=bias_row[0:1, :], in_=bkva[RANK : RANK + ROPE].rearrange("(r c) -> r c", r=1))
+
         hid_rows = {}
 
-        def load_hidden(first, count):
-            raw = inputs.tile([P, count * HID], BF16, name="hid_raw%d" % first)
-            nc.sync.dma_start(out=raw[:], in_=hid_dram[:, first * HID : (first + count) * HID])
-            for k in range(count):
-                hid_rows[first + k] = raw[:, k * HID : (k + 1) * HID]
+        def load_hidden(first, end):
+            raw = big.tile([P, (end - first) * HID], BF16, name="hid_raw%d" % first, offset=hid_at + first * HID * 2)
+            nc.sync.dma_start(out=raw[:], in_=hid_dram[:, first * HID : end * HID])
+            for i in range(first, end):
+                hid_rows[i] = raw[:, (i - first) * HID : (i - first + 1) * HID]
 
-        load_hidden(0, J // 2)
-        load_hidden(J // 2, J // 2)
-        raw_b = inputs.tile([P, PACK, HEADS * (NOPE + VDIM)], BF16)
-        half_cols = HALF_HEADS * (NOPE + VDIM)
-        for half in range(2):
-            cols = slice(half * half_cols, (half + 1) * half_cols)
-            nc.sync.dma_start(out=raw_b[:, :, cols], in_=wb_dram[:, :, cols])
-        load_hidden(J, J)
-        cos_sb = inputs.tile([P, GROUPS, J, ROPE], BF16)
-        sin_sb = inputs.tile([P, GROUPS, J, ROPE], BF16)
-        nc.sync.dma_start(out=cos_sb[:].rearrange("p g j d -> p (g j d)"), in_=cos_dram)
-        nc.sync.dma_start(out=sin_sb[:].rearrange("p g j d -> p (g j d)"), in_=sin_dram)
-        for g in range(2, GROUPS):
-            load_hidden(g * J, J)
+        load_hidden(0, 2)
+        raw_b = big.tile([P, PACK, HEADS, NOPE + VDIM], BF16, offset=raw_b_at)
+        nc.sync.dma_start(out=raw_b[:].rearrange("p t h x -> p (t h x)"), in_=wb_dram)
+        load_hidden(2, 4)
+        load_hidden(4, 8)
+        cos_sb = const.tile([P, TILES, ROPE], BF16)
+        sin_sb = const.tile([P, TILES, ROPE], BF16)
+        nc.sync.dma_start(out=cos_sb[:].rearrange("p s d -> p (s d)"), in_=cos_dram)
+        nc.sync.dma_start(out=sin_sb[:].rearrange("p s d -> p (s d)"), in_=sin_dram)
+        load_hidden(8, 12)
+        load_hidden(12, 16)
 
         ident_f32 = const.tile([P, P], F32)
         make_identity(nc, ident_f32[:])
@@ -109,43 +119,46 @@ def tile_gptossmlaattention_pa_kernel(tc, hidden_states, cos, sin, Wkva, bkva, W
 
         a_codes = const.tile([P, HID_PASSES, RANK + ROPE], U32, align_bytes=64)
         a_scales = const.tile([P, HID_PASSES, RANK + ROPE], U8, align_bytes=64)
-        grouped_a = []
-        for kp in range(HID_PASSES):
+
+        grouped_a = {}
+
+        def regroup_a(kp):
             grouped = wstage.tile([P, RANK + ROPE, PACK], BF16, align_bytes=64, name="grouped_a", tag="grouped")
-            nc.vector.tensor_copy(
-                out=grouped[:, 0:RANK, :].rearrange("p (b m) t -> p b m t", b=PACK),
-                in_=raw_a[:, kp, :, 0:RANK].rearrange("p t (m b) -> p b m t", b=PACK),
-            )
+            grouped_a[kp] = grouped
+            to = grouped[:, 0:RANK, :].rearrange("p (b m) t -> p b m t", b=PACK)
+            source = raw_a[:, kp, :, 0:RANK].rearrange("p t (m b) -> p b m t", b=PACK)
+            nc.vector.tensor_copy(out=to[:, 0:2], in_=source[:, 0:2])
+            nc.scalar.copy(out=to[:, 2:4], in_=source[:, 2:4])
             nc.vector.tensor_copy(
                 out=grouped[:, RANK:, :].rearrange("p (c i) t -> p c t i", i=4),
                 in_=raw_a[:, kp, :, RANK:].rearrange("p t (c i) -> p c t i", i=4),
             )
-            grouped_a.append(grouped)
-        for kp in range(HID_PASSES):
-            for cols in (slice(0, RANK), slice(RANK, RANK + ROPE)):
-                nc.vector.quantize_mx(
-                    out=a_codes[:, kp, cols].bitcast(FP8X4),
-                    scales=a_scales[:, kp, cols],
-                    in_=grouped_a[kp][:, cols, :].rearrange("p c t -> p (c t)"),
-                )
 
-        b_codes = const.tile([P, KV_CHUNKS * KV_CHUNK], U32, align_bytes=64)
-        b_scales = const.tile([P, KV_CHUNKS * KV_CHUNK], U8, align_bytes=64)
-        raw_b_heads = raw_b[:].rearrange("p t (h x) -> p t h x", x=NOPE + VDIM)
+        def quantise_a(kp, cols):
+            nc.vector.quantize_mx(
+                out=a_codes[:, kp, cols].bitcast(FP8X4),
+                scales=a_scales[:, kp, cols],
+                in_=grouped_a[kp][:, cols, :].rearrange("p c t -> p (c t)"),
+            )
+
+        b_codes = const.tile([P, 3 * KV_CHUNK], U32, align_bytes=64)
+        b_scales = const.tile([P, 3 * KV_CHUNK], U8, align_bytes=64)
         b_sources = [
-            raw_b_heads[:, :, 0:HALF_HEADS, NOPE:],
-            raw_b_heads[:, :, HALF_HEADS:HEADS, NOPE:],
-            raw_b_heads[:, :, :, 0:NOPE],
+            raw_b[:, :, 0:HALF_HEADS, NOPE:],
+            raw_b[:, :, HALF_HEADS:HEADS, NOPE:],
+            raw_b[:, :, :, 0:NOPE],
         ]
         grouped_b = {}
 
-        def regroup_b(n):
-            grouped_b[n] = wstage.tile([P, KV_CHUNK, PACK], BF16, align_bytes=64, name="grouped_b", tag="grouped")
-            copy = nc.scalar.copy if n < 2 else nc.vector.tensor_copy
-            copy(
-                out=grouped_b[n][:].rearrange("p (h d) t -> p h d t", h=b_sources[n].shape[2]),
-                in_=b_sources[n].rearrange("p t h d -> p h d t"),
-            )
+        def regroup_b(n, copies):
+            if n not in grouped_b:
+                grouped_b[n] = wstage.tile([P, KV_CHUNK, PACK], BF16, align_bytes=64, name="grouped_b", tag="grouped")
+            count = b_sources[n].shape[2]
+            to = grouped_b[n][:].rearrange("p (h d) t -> p h d t", h=count)
+            share = count // len(copies)
+            for k, copy in enumerate(copies):
+                heads = slice(k * share, (k + 1) * share)
+                copy(out=to[:, heads], in_=b_sources[n][:, :, heads, :].rearrange("p t h d -> p h d t"))
 
         def quantise_b(n):
             cols = slice(n * KV_CHUNK, (n + 1) * KV_CHUNK)
@@ -156,48 +169,57 @@ def tile_gptossmlaattention_pa_kernel(tc, hidden_states, cos, sin, Wkva, bkva, W
             )
 
         hid_q = {}
-        lat_q = {}
+        hid_raw = {}
+        xts = {}
+        kvs = {}
+        lat_codes = const.tile([P, TILES, P], U32, align_bytes=64)
+        lat_scales = const.tile([P, TILES, P], U8, align_bytes=64)
+        lat_ps = {}
+        lat_bf = {}
         rope_ps = {}
         rope_sb = {}
         kk_stage = {}
         v_stage = {}
 
-        def front(i):
+        def run_of(i, runs):
+            return [run for run in runs if run[0] <= i < run[1]][0]
+
+        def transpose_hidden(i):
             hid_words = hid_rows[i].bitcast(F32)
-            xt = psum_xt.tile([P, WORD_BLOCKS, P], F32, tag="xt")
-            for q in range(WORD_BLOCKS):
-                kp, u = divmod(q, 2)
-                nc.tensor.transpose(
-                    out=xt[:, q, :], in_=hid_words[:, 2 * P * kp + u : 2 * P * (kp + 1) : 2], identity=ident_f32[:]
-                )
-            hid_grouped = work.tile([P, HID_PASSES * P * PACK], BF16, align_bytes=64)
+            xt = psum_xt.tile([P, HID_PASSES, 2, P], F32, tag="xt")
+            for kp in range(HID_PASSES):
+                for u in range(2):
+                    nc.tensor.transpose(
+                        out=xt[:, kp, u, :], in_=hid_words[:, 2 * P * kp + u : 2 * P * (kp + 1) : 2], identity=ident_f32[:]
+                    )
+            xts[i] = xt
+
+        def empty_transposes(i):
+            xt = xts[i]
+            hid_raw[i] = work.tile([P, HID_PASSES * P * PACK], BF16, align_bytes=64, name="hid_grouped")
             nc.scalar.copy(
-                out=hid_grouped[:].bitcast(F32).rearrange("p (kp c u) -> p kp c u", kp=HID_PASSES, u=2),
-                in_=xt[:].rearrange("p (kp u) c -> p kp c u", u=2),
+                out=hid_raw[i][:].bitcast(F32).rearrange("p (kp c u) -> p kp c u", kp=HID_PASSES, u=2),
+                in_=xt[:].rearrange("p kp u c -> p kp c u"),
             )
+
+        def quantise_hidden(i):
             hid_codes = work.tile([P, HID_PASSES, P], U32, align_bytes=64)
             hid_scales = work.tile([P, HID_PASSES, P], U8, align_bytes=64)
             nc.vector.quantize_mx(
                 out=hid_codes[:].rearrange("p kp c -> p (kp c)").bitcast(FP8X4),
                 scales=hid_scales[:].rearrange("p kp c -> p (kp c)"),
-                in_=hid_grouped[:],
+                in_=hid_raw[i][:],
             )
             hid_q[i] = (hid_codes, hid_scales)
 
-        def middle(i):
-            g, j = divmod(i, J)
+        def first_matmul(i):
+            r, j = divmod(i, PAIR)
             hid_codes, hid_scales = hid_q[i]
-            if j == 0:
-                rope_ps[g] = psum_rope.tile([P, J, ROPE], F32, name="rope_ps")
-                lat_q[g] = (
-                    work.tile([P, J, P], U32, align_bytes=64, name="lat_codes"),
-                    work.tile([P, J, P], U8, align_bytes=64, name="lat_scales"),
-                )
-            lat_ps = psum_lat.tile([P, PACK, P], F32)
+            lat_ps[i] = psum_lat.tile([P, PACK, P], F32, name="lat_ps")
             for t in range(PACK):
                 for kp in range(HID_PASSES):
                     nc.tensor.matmul_mx(
-                        out=lat_ps[:, t, :],
+                        out=lat_ps[i][:, t, :],
                         lhsT=a_codes[:, kp, t * P : (t + 1) * P].bitcast(FP8X4),
                         lhsT_scale=a_scales[:, kp, t * P : (t + 1) * P],
                         rhs=hid_codes[:, kp, :].bitcast(FP8X4),
@@ -205,9 +227,11 @@ def tile_gptossmlaattention_pa_kernel(tc, hidden_states, cos, sin, Wkva, bkva, W
                         start=(kp == 0),
                         stop=(kp == HID_PASSES - 1),
                     )
+            if j == 0:
+                rope_ps[r] = psum_rope.tile([P, PAIR, ROPE], F32, name="rope_ps")
             for kp in range(HID_PASSES):
                 nc.tensor.matmul_mx(
-                    out=rope_ps[g][:, j, :],
+                    out=rope_ps[r][:, j, :],
                     lhsT=hid_codes[:, kp, :].bitcast(FP8X4),
                     lhsT_scale=hid_scales[:, kp, :],
                     rhs=a_codes[:, kp, RANK : RANK + ROPE].bitcast(FP8X4),
@@ -215,107 +239,208 @@ def tile_gptossmlaattention_pa_kernel(tc, hidden_states, cos, sin, Wkva, bkva, W
                     start=(kp == 0),
                     stop=(kp == HID_PASSES - 1),
                 )
-            lat_grouped = work.tile([P, P, PACK], BF16, align_bytes=64)
+
+        def add_latent_bias(i):
+            lat_bf[i] = work.tile([P, P, PACK], BF16, align_bytes=64, name="lat_grouped")
             nc.vector.tensor_tensor(
-                out=lat_grouped[:],
-                in0=lat_ps[:].rearrange("p t c -> p c t"),
+                out=lat_bf[i][:],
+                in0=lat_ps[i][:].rearrange("p t c -> p c t"),
                 in1=lat_bias[:].unsqueeze(1).to_broadcast([P, P, PACK]),
                 op=ADD,
             )
-            lat_codes, lat_scales = lat_q[g]
+
+        def quantise_latents(i):
             nc.vector.quantize_mx(
-                out=lat_codes[:, j, :].bitcast(FP8X4),
-                scales=lat_scales[:, j, :],
-                in_=lat_grouped[:].rearrange("p c t -> p (c t)"),
+                out=lat_codes[:, i, :].bitcast(FP8X4),
+                scales=lat_scales[:, i, :],
+                in_=lat_bf[i][:].rearrange("p c t -> p (c t)"),
             )
 
-        def rotate(g, part):
-            if part == 0:
-                kk_stage[g] = kk_pool.tile([P, HEADS, J, NOPE + ROPE], F32, name="kk_stage")
-                rope_sb[g] = (
-                    rope_pool.tile([P, J, ROPE], F32, name="k_rope"),
-                    rope_pool.tile([P, J, ROPE], F32, name="k_rot"),
-                    rope_pool.tile([P, J, ROPE], F32, name="crossed"),
+        def kk_tile(i):
+            first, end = run_of(i, K_RUNS)
+            if first not in kk_stage:
+                kk_stage[first] = big.tile(
+                    [P, HEADS, end - first, KDIM], F32, name="kk_stage%d" % first, offset=kk_at[first]
                 )
-            k_rope, k_rot, crossed = rope_sb[g]
+            return kk_stage[first], i - first
+
+        def rotate(r, part):
+            if part == 0:
+                rope_sb[r] = (
+                    rope_pool.tile([P, PAIR, ROPE], F32, name="k_rope"),
+                    rope_pool.tile([P, PAIR, ROPE], F32, name="k_rot"),
+                    rope_pool.tile([P, PAIR, ROPE], F32, name="crossed"),
+                )
+            k_rope, k_rot, crossed = rope_sb[r]
+            tiles = slice(r * PAIR, (r + 1) * PAIR)
             lo = slice(0, HALF_ROPE)
             hi = slice(HALF_ROPE, ROPE)
             if part == 0:
                 nc.vector.tensor_tensor(
                     out=k_rope[:],
-                    in0=rope_ps[g][:],
-                    in1=rope_bias[:].unsqueeze(1).to_broadcast([P, J, ROPE]),
+                    in0=rope_ps[r][:],
+                    in1=rope_bias[:].unsqueeze(1).to_broadcast([P, PAIR, ROPE]),
                     op=ADD,
                 )
             if part == 1:
-                nc.vector.tensor_tensor(out=k_rot[:], in0=k_rope[:], in1=cos_sb[:, g, :, :], op=MULT)
+                nc.vector.tensor_tensor(out=k_rot[:], in0=k_rope[:], in1=cos_sb[:, tiles, :], op=MULT)
                 nc.vector.scalar_tensor_tensor(
-                    out=crossed[:, :, lo], in0=k_rope[:, :, hi], scalar=-1.0, in1=sin_sb[:, g, :, lo], op0=MULT, op1=MULT
+                    out=crossed[:, :, lo], in0=k_rope[:, :, hi], scalar=-1.0, in1=sin_sb[:, tiles, lo], op0=MULT, op1=MULT
                 )
-                nc.vector.tensor_tensor(out=crossed[:, :, hi], in0=k_rope[:, :, lo], in1=sin_sb[:, g, :, hi], op=MULT)
+                nc.vector.tensor_tensor(out=crossed[:, :, hi], in0=k_rope[:, :, lo], in1=sin_sb[:, tiles, hi], op=MULT)
             if part == 2:
                 nc.vector.tensor_tensor(out=k_rot[:], in0=k_rot[:], in1=crossed[:], op=ADD)
-            if part >= 2:
-                heads = slice((part - 2) * HALF_HEADS, (part - 1) * HALF_HEADS)
+            if part >= 3:
+                heads = slice((part - 3) * HALF_HEADS, (part - 2) * HALF_HEADS)
+                stage, j = kk_tile(r * PAIR)
                 nc.vector.tensor_copy(
-                    out=kk_stage[g][:, heads, :, NOPE:],
-                    in_=k_rot[:].unsqueeze(1).to_broadcast([P, HALF_HEADS, J, ROPE]),
+                    out=stage[:, heads, j : j + PAIR, NOPE:],
+                    in_=k_rot[:].unsqueeze(1).to_broadcast([P, HALF_HEADS, PAIR, ROPE]),
                 )
 
-        def second(g, n, j):
-            together = [groups for groups in V_GROUPS if g in groups][0]
-            if n == 0 and j == 0 and g == together[0]:
-                tokens = len(together) * J
-                v_stage[g] = [
-                    v_pool.tile([P, HALF_HEADS, tokens, VDIM], F32, name="v_stage_%d_%d" % (g, half)) for half in range(2)
-                ]
-            lat_codes, lat_scales = lat_q[g]
+        def second(i, n):
             kv_ps = psum_kv.tile([P, KV_CHUNK], F32)
             cols = slice(n * KV_CHUNK, (n + 1) * KV_CHUNK)
             nc.tensor.matmul_mx(
                 out=kv_ps[:],
-                lhsT=lat_codes[:, j, :].bitcast(FP8X4),
-                lhsT_scale=lat_scales[:, j, :],
+                lhsT=lat_codes[:, i, :].bitcast(FP8X4),
+                lhsT_scale=lat_scales[:, i, :],
                 rhs=b_codes[:, cols].bitcast(FP8X4),
                 rhs_scale=b_scales[:, cols],
                 start=True,
                 stop=True,
             )
-            if n < 2:
-                stage = v_stage[together[0]][n]
-                nc.scalar.copy(
-                    out=stage[:, :, (g - together[0]) * J + j, :], in_=kv_ps[:].rearrange("p (h d) -> p h d", d=VDIM)
-                )
-                if j == J - 1 and g == together[-1]:
-                    heads = slice(n * HALF_HEADS, (n + 1) * HALF_HEADS)
-                    run = slice(together[0] * J * VDIM, (together[-1] + 1) * J * VDIM)
-                    nc.sync.dma_start(out=v_dram[:, heads, run], in_=stage[:].rearrange("p h j d -> p h (j d)"))
-            else:
-                nc.scalar.copy(out=kk_stage[g][:, :, j, 0:NOPE], in_=kv_ps[:].rearrange("p (h d) -> p h d", d=NOPE))
+            kvs[(i, n)] = kv_ps
 
-        def store_kk(g):
+        def empty_second(i, n, copy):
+            kv_ps = kvs[(i, n)]
+            if n == K_CHUNK:
+                stage, j = kk_tile(i)
+                copy(out=stage[:, :, j, 0:NOPE], in_=kv_ps[:].rearrange("p (h d) -> p h d", d=NOPE))
+            else:
+                first, end = run_of(i, V_RUNS)
+                if (first, n) not in v_stage:
+                    v_stage[(first, n)] = big.tile(
+                        [P, HALF_HEADS, end - first, VDIM], F32, name="v_stage%d_%d" % (first, n), offset=v_at[(first, n)]
+                    )
+                stage = v_stage[(first, n)]
+                copy(out=stage[:, :, i - first, :], in_=kv_ps[:].rearrange("p (h d) -> p h d", d=VDIM))
+
+        def store_values(run, half):
+            first, end = run
+            heads = slice(half * HALF_HEADS, (half + 1) * HALF_HEADS)
+            nc.sync.dma_start(
+                out=v_dram[:, heads, first * VDIM : end * VDIM],
+                in_=v_stage[(first, half)][:].rearrange("p h j d -> p h (j d)"),
+            )
+
+        def store_keys(run):
+            first, end = run
             for half in range(2):
                 heads = slice(half * HALF_HEADS, (half + 1) * HALF_HEADS)
                 nc.sync.dma_start(
-                    out=kk_dram[g, :, heads, :], in_=kk_stage[g][:, heads, :, :].rearrange("p h j d -> p h (j d)")
+                    out=kk_dram[:, heads, first * KDIM : end * KDIM],
+                    in_=kk_stage[first][:, heads, :, :].rearrange("p h j d -> p h (j d)"),
                 )
 
-        for s in range(TILES + GROUP_LAG):
-            if s % 2 == 0 and 1 <= s // 2 <= KV_CHUNKS:
-                quantise_b(s // 2 - 1)
-            if s >= GROUP_LAG:
-                g, quarter = divmod(s - GROUP_LAG, J)
-                for unit in range(KV_CHUNKS * quarter, KV_CHUNKS * (quarter + 1)):
-                    second(g, *divmod(unit, J))
-            if s < TILES:
-                front(s)
-            if s % 2 == 1 and s // 2 < KV_CHUNKS:
-                regroup_b(s // 2)
-            if s == 1:
-                spread_biases()
-            if 1 <= s <= TILES:
-                middle(s - 1)
-            if s >= GROUP_LAG:
-                rotate(g, quarter)
-                if quarter == J - 1:
-                    store_kk(g)
+        vector_copy = nc.vector.tensor_copy
+        scalar_copy = nc.scalar.copy
+        LATENT = slice(0, RANK)
+        ROPES = slice(RANK, RANK + ROPE)
+
+        with tc.manual_schedule():
+            def unit(i, n):
+                second(i, n)
+                empty_second(i, n, scalar_copy)
+
+            transpose_hidden(0)
+            transpose_hidden(1)
+            regroup_a(0)
+            quantise_a(0, LATENT)
+            regroup_a(1)
+            quantise_a(1, LATENT)
+            empty_transposes(0)
+            empty_transposes(1)
+            quantise_hidden(0)
+            quantise_a(0, ROPES)
+            quantise_a(1, ROPES)
+            quantise_hidden(1)
+            first_matmul(0)
+            first_matmul(1)
+            regroup_b(0, (vector_copy, scalar_copy))
+            add_latent_bias(0)
+            add_latent_bias(1)
+            quantise_b(0)
+            quantise_latents(0)
+            quantise_latents(1)
+            spread_biases()
+            rotate(0, 0)
+            transpose_hidden(2)
+            transpose_hidden(3)
+            regroup_b(1, (vector_copy, scalar_copy))
+            empty_transposes(2)
+            empty_transposes(3)
+            quantise_hidden(2)
+            quantise_hidden(3)
+            unit(0, 0)
+            unit(1, 0)
+            first_matmul(2)
+            first_matmul(3)
+            quantise_b(1)
+            add_latent_bias(2)
+            add_latent_bias(3)
+            rotate(1, 0)
+            quantise_latents(2)
+            quantise_latents(3)
+            regroup_b(K_CHUNK, (vector_copy, scalar_copy))
+            transpose_hidden(4)
+            transpose_hidden(5)
+            empty_transposes(4)
+            empty_transposes(5)
+            unit(2, 0)
+            unit(3, 0)
+            for i in range(4):
+                unit(i, 1)
+            rotate(0, 1)
+            quantise_b(K_CHUNK)
+            rotate(0, 2)
+            quantise_hidden(4)
+            rotate(0, 3)
+            rotate(0, 4)
+            store_values((0, 4), 0)
+            store_values((0, 4), 1)
+            for s in range(4, TILES + 2):
+                r, late = divmod(s - PAIR, PAIR)
+                q, j = divmod(s - 2, 4)
+                order = [(0, 0), (0, 1), (1, 0), (1, 1), (2, 0), (2, 1), (3, 0), (3, 1), (0, 2), (1, 2), (2, 2), (3, 2)]
+                units = [(4 * q + tile, n) for tile, n in order[3 * j : 3 * j + 3]]
+                if s == 4:
+                    units = [(0, 2), (1, 2)]
+                if s == 5:
+                    units = [(2, 2), (3, 2)]
+                if s < TILES:
+                    first_matmul(s)
+                if s + 2 < TILES:
+                    transpose_hidden(s + 2)
+                    empty_transposes(s + 2)
+                for i, n in units:
+                    unit(i, n)
+                if s + 1 < TILES:
+                    quantise_hidden(s + 1)
+                if r < PAIRS:
+                    rotate(r, 3 if late else 1)
+                if s < TILES:
+                    add_latent_bias(s)
+                if late and s < TILES:
+                    rotate(r + 1, 0)
+                if r < PAIRS:
+                    rotate(r, 4 if late else 2)
+                if s < TILES:
+                    quantise_latents(s)
+                for run in V_RUNS[1:]:
+                    if s == run[1]:
+                        store_values(run, 0)
+                        store_values(run, 1)
+                for run in K_RUNS:
+                    if s == run[1] + 1:
+                        store_keys(run)

@@ -348,7 +348,7 @@ def tile_gptossmlaattention_pa_kernel(tc, hidden_states, cos, sin, Wkva, bkva, W
         LATENT = slice(0, RANK)
         ROPES = slice(RANK, RANK + ROPE)
 
-        with tc.manual_schedule():
+        for region in range(1):
             def unit(i, n):
                 second(i, n)
                 empty_second(i, n, scalar_copy)

@@ -33,6 +33,7 @@ HALF_ROPE = ROPE // 2
 KV_CHUNK = 512
 K_CHUNK = 2
 
+SPANS = ((0, 4), (4, 8), (8, 16))
 K_RUNS = ((0, 4), (4, 8), (8, 12), (12, 16))
 V_RUNS = ((0, 4), (4, 8), (8, 16))
 
@@ -42,11 +43,14 @@ FLOPS = 2 * SEQ * HID * (RANK + ROPE) + 2 * SEQ * RANK * HEADS * (NOPE + VDIM)
 def tile_gptossmlaattention_pa_kernel(tc, hidden_states, cos, sin, Wkva, bkva, Wkvb, out_0, out_1):
     nc = tc.nc
 
-    hid_dram = hidden_states[0, :, :].rearrange("(p i) k -> p (i k)", p=P)
-    cos_dram = cos[0, :, :].rearrange("(p s) d -> p (s d)", p=P)
-    sin_dram = sin[0, :, :].rearrange("(p s) d -> p (s d)", p=P)
-    kk_dram = out_0[0, :, :, :].rearrange("h (p s) d -> p h (s d)", p=P)
-    v_dram = out_1[0, :, :, :].rearrange("h (p s) d -> p h (s d)", p=P)
+    def rows_of(tensor, span):
+        return tensor[span[0] * P : span[1] * P, :].rearrange("(p s) d -> p (s d)", p=P)
+
+    def head_rows_of(tensor, span):
+        return tensor[:, span[0] * P : span[1] * P, :].rearrange("h (p s) d -> p h (s d)", p=P)
+
+    def span_of(i):
+        return [span for span in SPANS if span[0] <= i < span[1]][0]
     wa_dram = Wkva.rearrange("(kp p t) c -> kp p (t c)", kp=HID_PASSES, p=P, t=PACK)
     wb_dram = Wkvb.rearrange("(p t) n -> p (t n)", t=PACK)
 
@@ -90,7 +94,9 @@ def tile_gptossmlaattention_pa_kernel(tc, hidden_states, cos, sin, Wkva, bkva, W
 
         def load_hidden(first, end):
             raw = big.tile([P, (end - first) * HID], BF16, name="hid_raw%d" % first, offset=hid_at + first * HID * 2)
-            nc.sync.dma_start(out=raw[:], in_=hid_dram[:, first * HID : end * HID])
+            span = span_of(first)
+            cols = slice((first - span[0]) * HID, (end - span[0]) * HID)
+            nc.sync.dma_start(out=raw[:], in_=rows_of(hidden_states[0, :, :], span)[:, cols])
             for i in range(first, end):
                 hid_rows[i] = raw[:, (i - first) * HID : (i - first + 1) * HID]
 
@@ -101,8 +107,12 @@ def tile_gptossmlaattention_pa_kernel(tc, hidden_states, cos, sin, Wkva, bkva, W
         load_hidden(4, 8)
         cos_sb = const.tile([P, TILES, ROPE], BF16)
         sin_sb = const.tile([P, TILES, ROPE], BF16)
-        nc.sync.dma_start(out=cos_sb[:].rearrange("p s d -> p (s d)"), in_=cos_dram)
-        nc.sync.dma_start(out=sin_sb[:].rearrange("p s d -> p (s d)"), in_=sin_dram)
+        for first, end in SPANS:
+            for table, source in ((cos_sb, cos), (sin_sb, sin)):
+                nc.sync.dma_start(
+                    out=table[:, first:end, :].rearrange("p s d -> p (s d)"),
+                    in_=rows_of(source[0, :, :], (first, end)),
+                )
         load_hidden(8, 12)
         load_hidden(12, 16)
 
@@ -329,17 +339,21 @@ def tile_gptossmlaattention_pa_kernel(tc, hidden_states, cos, sin, Wkva, bkva, W
         def store_values(run, half):
             first, end = run
             heads = slice(half * HALF_HEADS, (half + 1) * HALF_HEADS)
+            span = span_of(first)
+            cols = slice((first - span[0]) * VDIM, (end - span[0]) * VDIM)
             nc.sync.dma_start(
-                out=v_dram[:, heads, first * VDIM : end * VDIM],
+                out=head_rows_of(out_1[0, :, :, :], span)[:, heads, cols],
                 in_=v_stage[(first, half)][:].rearrange("p h j d -> p h (j d)"),
             )
 
         def store_keys(run):
             first, end = run
+            span = span_of(first)
+            cols = slice((first - span[0]) * KDIM, (end - span[0]) * KDIM)
             for half in range(2):
                 heads = slice(half * HALF_HEADS, (half + 1) * HALF_HEADS)
                 nc.sync.dma_start(
-                    out=kk_dram[:, heads, first * KDIM : end * KDIM],
+                    out=head_rows_of(out_0[0, :, :, :], span)[:, heads, cols],
                     in_=kk_stage[first][:, heads, :, :].rearrange("p h j d -> p h (j d)"),
                 )
 

@@ -83,7 +83,7 @@ def tile_gptossmlaattention_pa_kernel(tc, hidden_states, cos, sin, Wkva, bkva, W
 
         bias_row = const.tile([P, ROPE], BF16)
         nc.vector.memset(bias_row[:], 0.0)
-        raw_a = big.tile([P, HID_PASSES, PACK, RANK + ROPE], BF16, offset=raw_a_at)
+        raw_a = big.tile([P, HID_PASSES, PACK, RANK + ROPE], BF16, align_bytes=256, offset=raw_a_at)
         for kp in range(HID_PASSES):
             nc.sync.dma_start(out=raw_a[:, kp, :, :].rearrange("p t c -> p (t c)"), in_=wa_dram[kp])
         lat_bias = const.tile([P, PACK], BF16)
@@ -93,7 +93,7 @@ def tile_gptossmlaattention_pa_kernel(tc, hidden_states, cos, sin, Wkva, bkva, W
         hid_rows = {}
 
         def load_hidden(first, end):
-            raw = big.tile([P, (end - first) * HID], BF16, name="hid_raw%d" % first, offset=hid_at + first * HID * 2)
+            raw = big.tile([P, (end - first) * HID], BF16, name="hid_raw%d" % first, align_bytes=256, offset=hid_at + first * HID * 2)
             span = span_of(first)
             cols = slice((first - span[0]) * HID, (end - span[0]) * HID)
             nc.sync.dma_start(out=raw[:], in_=rows_of(hidden_states[0, :, :], span)[:, cols])
@@ -101,12 +101,12 @@ def tile_gptossmlaattention_pa_kernel(tc, hidden_states, cos, sin, Wkva, bkva, W
                 hid_rows[i] = raw[:, (i - first) * HID : (i - first + 1) * HID]
 
         load_hidden(0, 2)
-        raw_b = big.tile([P, PACK, HEADS, NOPE + VDIM], BF16, offset=raw_b_at)
+        raw_b = big.tile([P, PACK, HEADS, NOPE + VDIM], BF16, align_bytes=256, offset=raw_b_at)
         nc.sync.dma_start(out=raw_b[:].rearrange("p t h x -> p (t h x)"), in_=wb_dram)
         load_hidden(2, 4)
         load_hidden(4, 8)
-        cos_sb = const.tile([P, TILES, ROPE], BF16)
-        sin_sb = const.tile([P, TILES, ROPE], BF16)
+        cos_sb = const.tile([P, TILES, ROPE], BF16, align_bytes=256)
+        sin_sb = const.tile([P, TILES, ROPE], BF16, align_bytes=256)
         for first, end in SPANS:
             for table, source in ((cos_sb, cos), (sin_sb, sin)):
                 nc.sync.dma_start(
@@ -270,7 +270,7 @@ def tile_gptossmlaattention_pa_kernel(tc, hidden_states, cos, sin, Wkva, bkva, W
             first, end = run_of(i, K_RUNS)
             if first not in kk_stage:
                 kk_stage[first] = big.tile(
-                    [P, HEADS, end - first, KDIM], F32, name="kk_stage%d" % first, offset=kk_at[first]
+                    [P, HEADS, end - first, KDIM], F32, name="kk_stage%d" % first, align_bytes=256, offset=kk_at[first]
                 )
             return kk_stage[first], i - first
 
@@ -331,7 +331,7 @@ def tile_gptossmlaattention_pa_kernel(tc, hidden_states, cos, sin, Wkva, bkva, W
                 first, end = run_of(i, V_RUNS)
                 if (first, n) not in v_stage:
                     v_stage[(first, n)] = big.tile(
-                        [P, HALF_HEADS, end - first, VDIM], F32, name="v_stage%d_%d" % (first, n), offset=v_at[(first, n)]
+                        [P, HALF_HEADS, end - first, VDIM], F32, name="v_stage%d_%d" % (first, n), align_bytes=256, offset=v_at[(first, n)]
                     )
                 stage = v_stage[(first, n)]
                 copy(out=stage[:, :, i - first, :], in_=kv_ps[:].rearrange("p (h d) -> p h d", d=VDIM))

@@ -35,7 +35,7 @@ K_CHUNK = 2
 
 SPANS = ((0, 4), (4, 8), (8, 16))
 K_RUNS = ((0, 4), (4, 8), (8, 12), (12, 16))
-V_RUNS = ((0, 4), (4, 8), (8, 16))
+V_RUNS = ((0, 4), (4, 6), (6, 8), (8, 12), (12, 16))
 
 FLOPS = 2 * SEQ * HID * (RANK + ROPE) + 2 * SEQ * RANK * HEADS * (NOPE + VDIM)
 
@@ -72,25 +72,26 @@ def tile_gptossmlaattention_pa_kernel(tc, hidden_states, cos, sin, Wkva, bkva, W
         hid_at = raw_b_at + PACK * HEADS * (NOPE + VDIM) * 2
         at = hid_at + TILES * HID * 2
         kk_at = {}
-        for k, (first, end) in enumerate(K_RUNS):
-            kk_at[first] = at + k % 3 * 4 * KK_TILE
+        for first, end in K_RUNS:
+            kk_at[first] = at + first % 12 * KK_TILE
         at += 12 * KK_TILE
-        v_at = {(8, 0): raw_a_at, (8, 1): hid_at}
-        for first in (0, 4):
+        v_at = {}
+        for first, end in V_RUNS:
             for half in range(2):
-                v_at[(first, half)] = at
-                at += 4 * V_TILE
+                if first >= 8:
+                    v_at[(first, half)] = (raw_a_at, hid_at)[half] + (first - 8) * V_TILE
+                else:
+                    v_at[(first, half)] = at
+                    at += (end - first) * V_TILE
 
         bias_row = const.tile([P, ROPE], BF16)
         nc.vector.memset(bias_row[:], 0.0)
         raw_a = big.tile([P, HID_PASSES, PACK, RANK + ROPE], BF16, align_bytes=256, offset=raw_a_at)
-        for kp in range(HID_PASSES):
-            nc.sync.dma_start(out=raw_a[:, kp, :, :].rearrange("p t c -> p (t c)"), in_=wa_dram[kp])
         lat_bias = const.tile([P, PACK], BF16)
-        nc.sync.dma_start(out=lat_bias[:], in_=bkva[0:RANK].rearrange("(p t) -> p t", t=PACK))
-        nc.sync.dma_start(out=bias_row[0:1, :], in_=bkva[RANK : RANK + ROPE].rearrange("(r c) -> r c", r=1))
-
         hid_rows = {}
+        raw_b = big.tile([P, PACK, HEADS, NOPE + VDIM], BF16, align_bytes=256, offset=raw_b_at)
+        cos_sb = const.tile([P, TILES, ROPE], BF16, align_bytes=256)
+        sin_sb = const.tile([P, TILES, ROPE], BF16, align_bytes=256)
 
         def load_hidden(first, end):
             raw = big.tile([P, (end - first) * HID], BF16, name="hid_raw%d" % first, align_bytes=256, offset=hid_at + first * HID * 2)
@@ -100,20 +101,31 @@ def tile_gptossmlaattention_pa_kernel(tc, hidden_states, cos, sin, Wkva, bkva, W
             for i in range(first, end):
                 hid_rows[i] = raw[:, (i - first) * HID : (i - first + 1) * HID]
 
-        load_hidden(0, 2)
-        raw_b = big.tile([P, PACK, HEADS, NOPE + VDIM], BF16, align_bytes=256, offset=raw_b_at)
-        nc.sync.dma_start(out=raw_b[:].rearrange("p t h x -> p (t h x)"), in_=wb_dram)
-        load_hidden(2, 4)
-        load_hidden(4, 8)
-        cos_sb = const.tile([P, TILES, ROPE], BF16, align_bytes=256)
-        sin_sb = const.tile([P, TILES, ROPE], BF16, align_bytes=256)
-        for first, end in SPANS:
+        def load_a(kp):
+            nc.sync.dma_start(out=raw_a[:, kp, :, :].rearrange("p t c -> p (t c)"), in_=wa_dram[kp])
+
+        def load_biases():
+            nc.sync.dma_start(out=lat_bias[:], in_=bkva[0:RANK].rearrange("(p t) -> p t", t=PACK))
+            nc.sync.dma_start(out=bias_row[0:1, :], in_=bkva[RANK : RANK + ROPE].rearrange("(r c) -> r c", r=1))
+
+        def load_tables(first, end):
             for table, source in ((cos_sb, cos), (sin_sb, sin)):
                 nc.sync.dma_start(
                     out=table[:, first:end, :].rearrange("p s d -> p (s d)"),
                     in_=rows_of(source[0, :, :], (first, end)),
                 )
+
+        load_a(0)
+        load_a(1)
+        load_biases()
+        load_hidden(0, 2)
+        nc.sync.dma_start(out=raw_b[:].rearrange("p t h x -> p (t h x)"), in_=wb_dram)
+        load_hidden(2, 4)
+        load_tables(0, 4)
+        load_hidden(4, 8)
+        load_tables(4, 8)
         load_hidden(8, 12)
+        load_tables(8, 16)
         load_hidden(12, 16)
 
         ident_f32 = const.tile([P, P], F32)
@@ -123,9 +135,9 @@ def tile_gptossmlaattention_pa_kernel(tc, hidden_states, cos, sin, Wkva, bkva, W
         rope_bias = const.tile([P, ROPE], F32)
 
         def spread_biases():
-            rope_bias_ps = psum_xt.tile([P, ROPE], F32, tag="xt")
+            rope_bias_ps = psum_kv.tile([P, ROPE], F32, name="rope_bias_ps", tag="kv_ps")
             nc.tensor.matmul(out=rope_bias_ps[:], lhsT=ones[:], rhs=bias_row[:], start=True, stop=True)
-            nc.vector.tensor_copy(out=rope_bias[:], in_=rope_bias_ps[:])
+            return rope_bias_ps
 
         a_codes = const.tile([P, HID_PASSES, RANK + ROPE], U32, align_bytes=64)
         a_scales = const.tile([P, HID_PASSES, RANK + ROPE], U8, align_bytes=64)
@@ -309,7 +321,7 @@ def tile_gptossmlaattention_pa_kernel(tc, hidden_states, cos, sin, Wkva, bkva, W
                 )
 
         def second(i, n):
-            kv_ps = psum_kv.tile([P, KV_CHUNK], F32)
+            kv_ps = psum_kv.tile([P, KV_CHUNK], F32, name="kv_ps", tag="kv_ps")
             cols = slice(n * KV_CHUNK, (n + 1) * KV_CHUNK)
             nc.tensor.matmul_mx(
                 out=kv_ps[:],
@@ -362,13 +374,22 @@ def tile_gptossmlaattention_pa_kernel(tc, hidden_states, cos, sin, Wkva, bkva, W
         LATENT = slice(0, RANK)
         ROPES = slice(RANK, RANK + ROPE)
 
-        for region in range(1):
+        blank = const.tile([P, KV_CHUNK], BF16)
+        nc.vector.memset(blank[:], 0.0)
+        with tc.manual_schedule():
             def unit(i, n):
                 second(i, n)
                 empty_second(i, n, scalar_copy)
 
+            for k in range(14):
+                warm_ps = psum_kv.tile([P, KV_CHUNK], F32, name="warm_ps", tag="kv_ps")
+                nc.tensor.matmul(out=warm_ps[:], lhsT=ones[:], rhs=blank[:], start=True, stop=True)
             transpose_hidden(0)
             transpose_hidden(1)
+            rope_bias_ps = spread_biases()
+            for k in range(3):
+                warm_ps = psum_kv.tile([P, KV_CHUNK], F32, name="warm_ps", tag="kv_ps")
+                nc.tensor.matmul(out=warm_ps[:], lhsT=ones[:], rhs=blank[:], start=True, stop=True)
             regroup_a(0)
             quantise_a(0, LATENT)
             regroup_a(1)
@@ -379,21 +400,21 @@ def tile_gptossmlaattention_pa_kernel(tc, hidden_states, cos, sin, Wkva, bkva, W
             quantise_a(0, ROPES)
             quantise_a(1, ROPES)
             quantise_hidden(1)
+            nc.vector.tensor_copy(out=rope_bias[:], in_=rope_bias_ps[:])
             first_matmul(0)
             first_matmul(1)
-            regroup_b(0, (vector_copy, scalar_copy))
+            transpose_hidden(2)
+            transpose_hidden(3)
             add_latent_bias(0)
+            regroup_b(0, (vector_copy, scalar_copy))
+            empty_transposes(2)
+            empty_transposes(3)
             add_latent_bias(1)
             quantise_b(0)
             quantise_latents(0)
             quantise_latents(1)
-            spread_biases()
             rotate(0, 0)
-            transpose_hidden(2)
-            transpose_hidden(3)
             regroup_b(1, (vector_copy, scalar_copy))
-            empty_transposes(2)
-            empty_transposes(3)
             quantise_hidden(2)
             quantise_hidden(3)
             unit(0, 0)
@@ -407,31 +428,42 @@ def tile_gptossmlaattention_pa_kernel(tc, hidden_states, cos, sin, Wkva, bkva, W
             quantise_latents(2)
             quantise_latents(3)
             regroup_b(K_CHUNK, (vector_copy, scalar_copy))
+            unit(0, 1)
+            unit(1, 1)
             transpose_hidden(4)
-            transpose_hidden(5)
             empty_transposes(4)
-            empty_transposes(5)
-            unit(2, 0)
-            unit(3, 0)
-            for i in range(4):
-                unit(i, 1)
-            rotate(0, 1)
             quantise_b(K_CHUNK)
-            rotate(0, 2)
             quantise_hidden(4)
+            rotate(0, 1)
+            rotate(1, 1)
+            for i in (2, 3):
+                unit(i, 0)
+            store_values((0, 4), 0)
+            for i in (2, 3):
+                unit(i, 1)
+            store_values((0, 4), 1)
+            first_matmul(4)
+            rotate(0, 2)
+            rotate(1, 2)
+            unit(0, 2)
+            unit(1, 2)
+            transpose_hidden(5)
+            empty_transposes(5)
+            unit(2, 2)
+            unit(3, 2)
             rotate(0, 3)
             rotate(0, 4)
-            store_values((0, 4), 0)
-            store_values((0, 4), 1)
-            for s in range(4, TILES + 2):
+            rotate(1, 3)
+            quantise_hidden(5)
+            rotate(1, 4)
+            store_keys((0, 4))
+            transpose_hidden(6)
+            empty_transposes(6)
+            add_latent_bias(4)
+            quantise_latents(4)
+            for s in range(5, TILES + 2):
                 r, late = divmod(s - PAIR, PAIR)
-                q, j = divmod(s - 2, 4)
-                order = [(0, 0), (0, 1), (1, 0), (1, 1), (2, 0), (2, 1), (3, 0), (3, 1), (0, 2), (1, 2), (2, 2), (3, 2)]
-                units = [(4 * q + tile, n) for tile, n in order[3 * j : 3 * j + 3]]
-                if s == 4:
-                    units = [(0, 2), (1, 2)]
-                if s == 5:
-                    units = [(2, 2), (3, 2)]
+                units = [(s - 1, n) for n in range(3)] if s <= TILES else []
                 if s < TILES:
                     first_matmul(s)
                 if s + 2 < TILES:
@@ -441,13 +473,13 @@ def tile_gptossmlaattention_pa_kernel(tc, hidden_states, cos, sin, Wkva, bkva, W
                     unit(i, n)
                 if s + 1 < TILES:
                     quantise_hidden(s + 1)
-                if r < PAIRS:
+                if r < PAIRS and s > 5:
                     rotate(r, 3 if late else 1)
                 if s < TILES:
                     add_latent_bias(s)
                 if late and s < TILES:
                     rotate(r + 1, 0)
-                if r < PAIRS:
+                if r < PAIRS and s > 5:
                     rotate(r, 4 if late else 2)
                 if s < TILES:
                     quantise_latents(s)
@@ -455,6 +487,6 @@ def tile_gptossmlaattention_pa_kernel(tc, hidden_states, cos, sin, Wkva, bkva, W
                     if s == run[1]:
                         store_values(run, 0)
                         store_values(run, 1)
-                for run in K_RUNS:
+                for run in K_RUNS[1:]:
                     if s == run[1] + 1:
                         store_keys(run)

@@ -33,9 +33,9 @@ HALF_ROPE = ROPE // 2
 KV_CHUNK = 512
 K_CHUNK = 2
 
-SPANS = ((0, 4), (4, 8), (8, 16))
-K_RUNS = ((0, 4), (4, 8), (8, 12), (12, 16))
-V_RUNS = ((0, 4), (4, 6), (6, 8), (8, 12), (12, 16))
+SPANS = ((0, 8), (8, 16))
+K_RUNS = ((0, 2), (2, 4), (4, 6), (6, 8), (8, 12), (12, 16))
+V_RUNS = ((0, 2), (2, 4), (4, 6), (6, 8), (8, 10), (10, 12), (12, 16))
 
 FLOPS = 2 * SEQ * HID * (RANK + ROPE) + 2 * SEQ * RANK * HEADS * (NOPE + VDIM)
 
@@ -66,7 +66,7 @@ def tile_gptossmlaattention_pa_kernel(tc, hidden_states, cos, sin, Wkva, bkva, W
         psum_kv = ctx.enter_context(tc.psum_pool(name="psum_kv", bufs=3))
 
         KK_TILE = HEADS * KDIM * 4
-        V_TILE = HALF_HEADS * VDIM * 4
+        V_TILE = HEADS * VDIM * 4
         raw_a_at = 0
         raw_b_at = raw_a_at + HID_PASSES * PACK * (RANK + ROPE) * 2
         hid_at = raw_b_at + PACK * HEADS * (NOPE + VDIM) * 2
@@ -77,17 +77,19 @@ def tile_gptossmlaattention_pa_kernel(tc, hidden_states, cos, sin, Wkva, bkva, W
         at += 12 * KK_TILE
         v_at = {}
         for first, end in V_RUNS:
-            for half in range(2):
-                if first >= 8:
-                    v_at[(first, half)] = (raw_a_at, hid_at)[half] + (first - 8) * V_TILE
-                else:
-                    v_at[(first, half)] = at
-                    at += (end - first) * V_TILE
+            if first < 8:
+                v_at[first] = at
+                at += (end - first) * V_TILE
+            else:
+                v_at[first] = (raw_a_at if first < 12 else hid_at) + first % 4 * V_TILE
 
-        bias_row = const.tile([P, ROPE], BF16)
+        ones = const.tile([P, P], BF16)
+        nc.vector.memset(ones[:], 1.0)
+        blank = const.tile([P, KV_CHUNK], BF16)
+        nc.vector.memset(blank[:], 0.0)
+        bias_row = const.tile([P, RANK + ROPE], BF16)
         nc.vector.memset(bias_row[:], 0.0)
         raw_a = big.tile([P, HID_PASSES, PACK, RANK + ROPE], BF16, align_bytes=256, offset=raw_a_at)
-        lat_bias = const.tile([P, PACK], BF16)
         hid_rows = {}
         raw_b = big.tile([P, PACK, HEADS, NOPE + VDIM], BF16, align_bytes=256, offset=raw_b_at)
         cos_sb = const.tile([P, TILES, ROPE], BF16, align_bytes=256)
@@ -105,8 +107,7 @@ def tile_gptossmlaattention_pa_kernel(tc, hidden_states, cos, sin, Wkva, bkva, W
             nc.sync.dma_start(out=raw_a[:, kp, :, :].rearrange("p t c -> p (t c)"), in_=wa_dram[kp])
 
         def load_biases():
-            nc.sync.dma_start(out=lat_bias[:], in_=bkva[0:RANK].rearrange("(p t) -> p t", t=PACK))
-            nc.sync.dma_start(out=bias_row[0:1, :], in_=bkva[RANK : RANK + ROPE].rearrange("(r c) -> r c", r=1))
+            nc.sync.dma_start(out=bias_row[0:1, :], in_=bkva.rearrange("(r c) -> r c", r=1))
 
         def load_tables(first, end):
             for table, source in ((cos_sb, cos), (sin_sb, sin)):
@@ -121,23 +122,29 @@ def tile_gptossmlaattention_pa_kernel(tc, hidden_states, cos, sin, Wkva, bkva, W
         load_hidden(0, 2)
         nc.sync.dma_start(out=raw_b[:].rearrange("p t h x -> p (t h x)"), in_=wb_dram)
         load_hidden(2, 4)
-        load_tables(0, 4)
+        load_tables(0, 8)
         load_hidden(4, 8)
-        load_tables(4, 8)
-        load_hidden(8, 12)
         load_tables(8, 16)
-        load_hidden(12, 16)
+        load_hidden(8, 16)
 
         ident_f32 = const.tile([P, P], F32)
         make_identity(nc, ident_f32[:])
-        ones = const.tile([P, P], BF16)
-        nc.vector.memset(ones[:], 1.0)
-        rope_bias = const.tile([P, ROPE], F32)
+        biases = const.tile([P, ROPE + PACK], F32)
+        rope_bias = biases[:, 0:ROPE]
+        lat_bias = biases[:, ROPE:]
 
         def spread_biases():
-            rope_bias_ps = psum_kv.tile([P, ROPE], F32, name="rope_bias_ps", tag="kv_ps")
-            nc.tensor.matmul(out=rope_bias_ps[:], lhsT=ones[:], rhs=bias_row[:], start=True, stop=True)
-            return rope_bias_ps
+            bias_ps = psum_kv.tile([P, ROPE + PACK], F32, name="bias_ps", tag="kv_ps")
+            nc.tensor.matmul(out=bias_ps[:, 0:ROPE], lhsT=ones[:], rhs=bias_row[:, RANK:], start=True, stop=True)
+            for t in range(PACK):
+                nc.tensor.matmul(
+                    out=bias_ps[:, ROPE + t : ROPE + t + 1],
+                    lhsT=bias_row[:, t:RANK:PACK],
+                    rhs=ones[:, 0:1],
+                    start=True,
+                    stop=True,
+                )
+            return bias_ps
 
         a_codes = const.tile([P, HID_PASSES, RANK + ROPE], U32, align_bytes=64)
         a_scales = const.tile([P, HID_PASSES, RANK + ROPE], U8, align_bytes=64)
@@ -267,7 +274,7 @@ def tile_gptossmlaattention_pa_kernel(tc, hidden_states, cos, sin, Wkva, bkva, W
             nc.vector.tensor_tensor(
                 out=lat_bf[i][:],
                 in0=lat_ps[i][:].rearrange("p t c -> p c t"),
-                in1=lat_bias[:].unsqueeze(1).to_broadcast([P, P, PACK]),
+                in1=lat_bias.unsqueeze(1).to_broadcast([P, P, PACK]),
                 op=ADD,
             )
 
@@ -301,7 +308,7 @@ def tile_gptossmlaattention_pa_kernel(tc, hidden_states, cos, sin, Wkva, bkva, W
                 nc.vector.tensor_tensor(
                     out=k_rope[:],
                     in0=rope_ps[r][:],
-                    in1=rope_bias[:].unsqueeze(1).to_broadcast([P, PAIR, ROPE]),
+                    in1=rope_bias.unsqueeze(1).to_broadcast([P, PAIR, ROPE]),
                     op=ADD,
                 )
             if part == 1:
@@ -341,41 +348,30 @@ def tile_gptossmlaattention_pa_kernel(tc, hidden_states, cos, sin, Wkva, bkva, W
                 copy(out=stage[:, :, j, 0:NOPE], in_=kv_ps[:].rearrange("p (h d) -> p h d", d=NOPE))
             else:
                 first, end = run_of(i, V_RUNS)
-                if (first, n) not in v_stage:
-                    v_stage[(first, n)] = big.tile(
-                        [P, HALF_HEADS, end - first, VDIM], F32, name="v_stage%d_%d" % (first, n), align_bytes=256, offset=v_at[(first, n)]
+                if first not in v_stage:
+                    v_stage[first] = big.tile(
+                        [P, HEADS, end - first, VDIM], F32, name="v_stage%d" % first, align_bytes=256, offset=v_at[first]
                     )
-                stage = v_stage[(first, n)]
-                copy(out=stage[:, :, i - first, :], in_=kv_ps[:].rearrange("p (h d) -> p h d", d=VDIM))
+                heads = slice(n * HALF_HEADS, (n + 1) * HALF_HEADS)
+                copy(out=v_stage[first][:, heads, i - first, :], in_=kv_ps[:].rearrange("p (h d) -> p h d", d=VDIM))
 
-        def store_values(run, half):
+        def store(dram, stage, run, d, heads):
             first, end = run
-            heads = slice(half * HALF_HEADS, (half + 1) * HALF_HEADS)
             span = span_of(first)
-            cols = slice((first - span[0]) * VDIM, (end - span[0]) * VDIM)
+            cols = slice((first - span[0]) * d, (end - span[0]) * d)
             nc.sync.dma_start(
-                out=head_rows_of(out_1[0, :, :, :], span)[:, heads, cols],
-                in_=v_stage[(first, half)][:].rearrange("p h j d -> p h (j d)"),
+                out=head_rows_of(dram[0, :, :, :], span)[:, heads, cols],
+                in_=stage[first][:, heads, :, :].rearrange("p h j d -> p h (j d)"),
             )
 
-        def store_keys(run):
-            first, end = run
-            span = span_of(first)
-            cols = slice((first - span[0]) * KDIM, (end - span[0]) * KDIM)
-            for half in range(2):
-                heads = slice(half * HALF_HEADS, (half + 1) * HALF_HEADS)
-                nc.sync.dma_start(
-                    out=head_rows_of(out_0[0, :, :, :], span)[:, heads, cols],
-                    in_=kk_stage[first][:, heads, :, :].rearrange("p h j d -> p h (j d)"),
-                )
+        HALVES = (slice(0, HALF_HEADS), slice(HALF_HEADS, HEADS))
+        ALL = slice(0, HEADS)
 
         vector_copy = nc.vector.tensor_copy
         scalar_copy = nc.scalar.copy
         LATENT = slice(0, RANK)
         ROPES = slice(RANK, RANK + ROPE)
 
-        blank = const.tile([P, KV_CHUNK], BF16)
-        nc.vector.memset(blank[:], 0.0)
         with tc.manual_schedule():
             def unit(i, n):
                 second(i, n)
@@ -386,7 +382,7 @@ def tile_gptossmlaattention_pa_kernel(tc, hidden_states, cos, sin, Wkva, bkva, W
                 nc.tensor.matmul(out=warm_ps[:], lhsT=ones[:], rhs=blank[:], start=True, stop=True)
             transpose_hidden(0)
             transpose_hidden(1)
-            rope_bias_ps = spread_biases()
+            bias_ps = spread_biases()
             for k in range(3):
                 warm_ps = psum_kv.tile([P, KV_CHUNK], F32, name="warm_ps", tag="kv_ps")
                 nc.tensor.matmul(out=warm_ps[:], lhsT=ones[:], rhs=blank[:], start=True, stop=True)
@@ -400,7 +396,7 @@ def tile_gptossmlaattention_pa_kernel(tc, hidden_states, cos, sin, Wkva, bkva, W
             quantise_a(0, ROPES)
             quantise_a(1, ROPES)
             quantise_hidden(1)
-            nc.vector.tensor_copy(out=rope_bias[:], in_=rope_bias_ps[:])
+            nc.vector.tensor_copy(out=biases[:], in_=bias_ps[:])
             first_matmul(0)
             first_matmul(1)
             transpose_hidden(2)
@@ -427,49 +423,58 @@ def tile_gptossmlaattention_pa_kernel(tc, hidden_states, cos, sin, Wkva, bkva, W
             rotate(1, 0)
             quantise_latents(2)
             quantise_latents(3)
-            regroup_b(K_CHUNK, (vector_copy, scalar_copy))
+            regroup_b(K_CHUNK, (vector_copy,))
             unit(0, 1)
             unit(1, 1)
+            store(out_1, v_stage, (0, 2), VDIM, ALL)
             transpose_hidden(4)
             empty_transposes(4)
-            quantise_b(K_CHUNK)
             quantise_hidden(4)
-            rotate(0, 1)
-            rotate(1, 1)
+            quantise_b(K_CHUNK)
             for i in (2, 3):
                 unit(i, 0)
-            store_values((0, 4), 0)
-            for i in (2, 3):
-                unit(i, 1)
-            store_values((0, 4), 1)
-            first_matmul(4)
-            rotate(0, 2)
-            rotate(1, 2)
-            unit(0, 2)
-            unit(1, 2)
+            store(out_1, v_stage, (2, 4), VDIM, HALVES[0])
             transpose_hidden(5)
             empty_transposes(5)
-            unit(2, 2)
-            unit(3, 2)
-            rotate(0, 3)
-            rotate(0, 4)
-            rotate(1, 3)
-            quantise_hidden(5)
-            rotate(1, 4)
-            store_keys((0, 4))
+            for i in (2, 3):
+                unit(i, 1)
+            store(out_1, v_stage, (2, 4), VDIM, HALVES[1])
+            first_matmul(4)
+            unit(0, 2)
+            unit(1, 2)
             transpose_hidden(6)
             empty_transposes(6)
+            unit(2, 2)
+            unit(3, 2)
+            rotate(0, 1)
+            rotate(1, 1)
+            rotate(0, 2)
+            quantise_hidden(5)
+            rotate(0, 3)
+            rotate(0, 4)
+            store(out_0, kk_stage, (0, 2), KDIM, ALL)
             add_latent_bias(4)
+            rotate(1, 2)
             quantise_latents(4)
+            rotate(1, 3)
+            rotate(1, 4)
+            store(out_0, kk_stage, (2, 4), KDIM, ALL)
             for s in range(5, TILES + 2):
                 r, late = divmod(s - PAIR, PAIR)
-                units = [(s - 1, n) for n in range(3)] if s <= TILES else []
+                units = [(s - 1, 0), (s - 1, 1)] if s <= TILES else []
+                if s > 5:
+                    units.append((s - 2, K_CHUNK))
                 if s < TILES:
                     first_matmul(s)
+                ahead = 0 if s == 5 else 1
+                for i, n in units[:ahead]:
+                    unit(i, n)
+                if s % 2 == 1:
+                    for i in range(s + 2, min(s + 4, TILES)):
+                        transpose_hidden(i)
                 if s + 2 < TILES:
-                    transpose_hidden(s + 2)
                     empty_transposes(s + 2)
-                for i, n in units:
+                for i, n in units[ahead:]:
                     unit(i, n)
                 if s + 1 < TILES:
                     quantise_hidden(s + 1)
@@ -483,10 +488,9 @@ def tile_gptossmlaattention_pa_kernel(tc, hidden_states, cos, sin, Wkva, bkva, W
                     rotate(r, 4 if late else 2)
                 if s < TILES:
                     quantise_latents(s)
-                for run in V_RUNS[1:]:
+                for run in V_RUNS[2:]:
                     if s == run[1]:
-                        store_values(run, 0)
-                        store_values(run, 1)
-                for run in K_RUNS[1:]:
+                        store(out_1, v_stage, run, VDIM, ALL)
+                for run in K_RUNS[2:]:
                     if s == run[1] + 1:
-                        store_keys(run)
+                        store(out_0, kk_stage, run, KDIM, ALL)

@@ -179,15 +179,11 @@ def tile_gptossmlaattention_pa_kernel(tc, hidden_states, cos, sin, Wkva, bkva, W
         ]
         grouped_b = {}
 
-        def regroup_b(n, copies):
+        def regroup_b(n, copy, first, end):
             if n not in grouped_b:
                 grouped_b[n] = wstage.tile([P, KV_CHUNK, PACK], BF16, align_bytes=64, name="grouped_b", tag="grouped")
-            count = b_sources[n].shape[2]
-            to = grouped_b[n][:].rearrange("p (h d) t -> p h d t", h=count)
-            share = count // len(copies)
-            for k, copy in enumerate(copies):
-                heads = slice(k * share, (k + 1) * share)
-                copy(out=to[:, heads], in_=b_sources[n][:, :, heads, :].rearrange("p t h d -> p h d t"))
+            to = grouped_b[n][:].rearrange("p (h d) t -> p h d t", h=b_sources[n].shape[2])
+            copy(out=to[:, first:end], in_=b_sources[n][:, :, first:end, :].rearrange("p t h d -> p h d t"))
 
         def quantise_b(n):
             cols = slice(n * KV_CHUNK, (n + 1) * KV_CHUNK)
@@ -318,13 +314,16 @@ def tile_gptossmlaattention_pa_kernel(tc, hidden_states, cos, sin, Wkva, bkva, W
                 )
                 nc.vector.tensor_tensor(out=crossed[:, :, hi], in0=k_rope[:, :, lo], in1=sin_sb[:, tiles, hi], op=MULT)
             if part == 2:
-                nc.vector.tensor_tensor(out=k_rot[:], in0=k_rot[:], in1=crossed[:], op=ADD)
-            if part >= 3:
-                heads = slice((part - 3) * HALF_HEADS, (part - 2) * HALF_HEADS)
                 stage, j = kk_tile(r * PAIR)
+                nc.vector.tensor_tensor(out=stage[:, 0, j : j + PAIR, NOPE:], in0=k_rot[:], in1=crossed[:], op=ADD)
+            if part >= 3:
+                stage, j = kk_tile(r * PAIR)
+                heads = slice(1, HALF_HEADS) if part == 3 else slice(HALF_HEADS, HEADS)
                 nc.vector.tensor_copy(
                     out=stage[:, heads, j : j + PAIR, NOPE:],
-                    in_=k_rot[:].unsqueeze(1).to_broadcast([P, HALF_HEADS, PAIR, ROPE]),
+                    in_=stage[:, 0, j : j + PAIR, NOPE:]
+                    .unsqueeze(1)
+                    .to_broadcast([P, heads.stop - heads.start, PAIR, ROPE]),
                 )
 
         def second(i, n):
@@ -402,16 +401,19 @@ def tile_gptossmlaattention_pa_kernel(tc, hidden_states, cos, sin, Wkva, bkva, W
             transpose_hidden(2)
             transpose_hidden(3)
             add_latent_bias(0)
-            regroup_b(0, (vector_copy, scalar_copy))
+            regroup_b(0, vector_copy, 0, 2)
+            regroup_b(0, scalar_copy, 2, 4)
+            regroup_b(2, scalar_copy, 6, 8)
             empty_transposes(2)
             empty_transposes(3)
+            regroup_b(1, scalar_copy, 2, 4)
             add_latent_bias(1)
             quantise_b(0)
             quantise_latents(0)
             quantise_latents(1)
             rotate(0, 0)
-            regroup_b(1, (vector_copy, scalar_copy))
             quantise_hidden(2)
+            regroup_b(1, vector_copy, 0, 2)
             quantise_hidden(3)
             unit(0, 0)
             unit(1, 0)
@@ -423,10 +425,11 @@ def tile_gptossmlaattention_pa_kernel(tc, hidden_states, cos, sin, Wkva, bkva, W
             rotate(1, 0)
             quantise_latents(2)
             quantise_latents(3)
-            regroup_b(K_CHUNK, (vector_copy,))
+            regroup_b(2, vector_copy, 0, 6)
+            store(out_1, v_stage, (0, 2), VDIM, HALVES[0])
             unit(0, 1)
             unit(1, 1)
-            store(out_1, v_stage, (0, 2), VDIM, ALL)
+            store(out_1, v_stage, (0, 2), VDIM, HALVES[1])
             transpose_hidden(4)
             empty_transposes(4)
             quantise_hidden(4)
@@ -451,8 +454,9 @@ def tile_gptossmlaattention_pa_kernel(tc, hidden_states, cos, sin, Wkva, bkva, W
             rotate(0, 2)
             quantise_hidden(5)
             rotate(0, 3)
+            store(out_0, kk_stage, (0, 2), KDIM, HALVES[0])
             rotate(0, 4)
-            store(out_0, kk_stage, (0, 2), KDIM, ALL)
+            store(out_0, kk_stage, (0, 2), KDIM, HALVES[1])
             add_latent_bias(4)
             rotate(1, 2)
             quantise_latents(4)

@@ -354,14 +354,17 @@ def tile_gptossmlaattention_pa_kernel(tc, hidden_states, cos, sin, Wkva, bkva, W
                 heads = slice(n * HALF_HEADS, (n + 1) * HALF_HEADS)
                 copy(out=v_stage[first][:, heads, i - first, :], in_=kv_ps[:].rearrange("p (h d) -> p h d", d=VDIM))
 
-        def store(dram, stage, run, d, heads):
+        def store(dram, stage, run, d, heads, pieces=1):
             first, end = run
             span = span_of(first)
-            cols = slice((first - span[0]) * d, (end - span[0]) * d)
-            nc.sync.dma_start(
-                out=head_rows_of(dram[0, :, :, :], span)[:, heads, cols],
-                in_=stage[first][:, heads, :, :].rearrange("p h j d -> p h (j d)"),
-            )
+            at = (first - span[0]) * d
+            whole = (end - first) * d
+            cuts = (0, whole) if pieces == 1 else (0, whole * 2 // 3, whole)
+            for lo, hi in zip(cuts, cuts[1:]):
+                nc.sync.dma_start(
+                    out=head_rows_of(dram[0, :, :, :], span)[:, heads, at + lo : at + hi],
+                    in_=stage[first][:, heads, :, :].rearrange("p h j d -> p h (j d)")[:, :, lo:hi],
+                )
 
         HALVES = (slice(0, HALF_HEADS), slice(HALF_HEADS, HEADS))
         ALL = slice(0, HEADS)
@@ -462,7 +465,7 @@ def tile_gptossmlaattention_pa_kernel(tc, hidden_states, cos, sin, Wkva, bkva, W
             quantise_latents(4)
             rotate(1, 3)
             rotate(1, 4)
-            store(out_0, kk_stage, (2, 4), KDIM, ALL)
+            store(out_0, kk_stage, (2, 4), KDIM, ALL, 2)
             for s in range(5, TILES + 2):
                 r, late = divmod(s - PAIR, PAIR)
                 units = [(s - 1, 0), (s - 1, 1)] if s <= TILES else []
@@ -497,4 +500,4 @@ def tile_gptossmlaattention_pa_kernel(tc, hidden_states, cos, sin, Wkva, bkva, W
                         store(out_1, v_stage, run, VDIM, ALL)
                 for run in K_RUNS[2:]:
                     if s == run[1] + 1:
-                        store(out_0, kk_stage, run, KDIM, ALL)
+                        store(out_0, kk_stage, run, KDIM, ALL, 2)

from contextlib import ExitStack

import concourse.mybir as mybir
from concourse.masks import make_identity

F32 = mybir.dt.float32
BF16 = mybir.dt.bfloat16
U32 = mybir.dt.uint32
U8 = mybir.dt.uint8
FP8X4 = mybir.dt.float8_e4m3fn_x4
ADD = mybir.AluOpType.add
MULT = mybir.AluOpType.mult

P = 128
PACK = 4
K_PASS = P * PACK

SEQ = 2048
HID = 1024
HEADS = 8
NOPE = 64
ROPE = 128
VDIM = 128
RANK = 512
KDIM = NOPE + ROPE

HID_PASSES = HID // K_PASS
TILES = SEQ // P
PAIR = 2
PAIRS = TILES // PAIR
HALF_HEADS = HEADS // 2
HALF_ROPE = ROPE // 2
KV_CHUNK = 512
K_CHUNK = 2

SPANS = ((0, 8), (8, 16))
K_RUNS = ((0, 2), (2, 4), (4, 6), (6, 8), (8, 12), (12, 16))
V_RUNS = ((0, 2), (2, 4), (4, 6), (6, 8), (8, 10), (10, 12), (12, 16))

FLOPS = 2 * SEQ * HID * (RANK + ROPE) + 2 * SEQ * RANK * HEADS * (NOPE + VDIM)


def tile_gptossmlaattention_pa_kernel(tc, hidden_states, cos, sin, Wkva, bkva, Wkvb, out_0, out_1):
    nc = tc.nc

    def rows_of(tensor, span):
        return tensor[span[0] * P : span[1] * P, :].rearrange("(p s) d -> p (s d)", p=P)

    def head_rows_of(tensor, span):
        return tensor[:, span[0] * P : span[1] * P, :].rearrange("h (p s) d -> p h (s d)", p=P)

    def span_of(i):
        return [span for span in SPANS if span[0] <= i < span[1]][0]
    wa_dram = Wkva.rearrange("(kp p t) c -> kp p (t c)", kp=HID_PASSES, p=P, t=PACK)
    wb_dram = Wkvb.rearrange("(p t) n -> p (t n)", t=PACK)

    with ExitStack() as ctx:
        const = ctx.enter_context(tc.tile_pool(name="const", bufs=1))
        big = ctx.enter_context(tc.tile_pool(name="big", bufs=1))
        wstage = ctx.enter_context(tc.tile_pool(name="wstage", bufs=3))
        work = ctx.enter_context(tc.tile_pool(name="work", bufs=3))
        rope_pool = ctx.enter_context(tc.tile_pool(name="rope", bufs=2))
        psum_xt = ctx.enter_context(tc.psum_pool(name="psum_xt", bufs=2))
        psum_lat = ctx.enter_context(tc.psum_pool(name="psum_lat", bufs=2))
        psum_rope = ctx.enter_context(tc.psum_pool(name="psum_rope", bufs=1))
        psum_kv = ctx.enter_context(tc.psum_pool(name="psum_kv", bufs=3))

        KK_TILE = HEADS * KDIM * 4
        V_TILE = HEADS * VDIM * 4
        raw_a_at = 0
        raw_b_at = raw_a_at + HID_PASSES * PACK * (RANK + ROPE) * 2
        hid_at = raw_b_at + PACK * HEADS * (NOPE + VDIM) * 2
        at = hid_at + TILES * HID * 2
        kk_at = {}
        for first, end in K_RUNS:
            kk_at[first] = at + first % 12 * KK_TILE
        at += 12 * KK_TILE
        v_at = {}
        for first, end in V_RUNS:
            if first < 8:
                v_at[first] = at
                at += (end - first) * V_TILE
            else:
                v_at[first] = (raw_a_at if first < 12 else hid_at) + first % 4 * V_TILE

        ones = const.tile([P, P], BF16)
        nc.vector.memset(ones[:], 1.0)
        blank = const.tile([P, KV_CHUNK], BF16)
        nc.vector.memset(blank[:], 0.0)
        bias_row = const.tile([P, RANK + ROPE], BF16)
        nc.vector.memset(bias_row[:], 0.0)
        raw_a = big.tile([P, HID_PASSES, PACK, RANK + ROPE], BF16, align_bytes=256, offset=raw_a_at)
        hid_rows = {}
        raw_b = big.tile([P, PACK, HEADS, NOPE + VDIM], BF16, align_bytes=256, offset=raw_b_at)
        cos_sb = const.tile([P, TILES, ROPE], BF16, align_bytes=256)
        sin_sb = const.tile([P, TILES, ROPE], BF16, align_bytes=256)

        def load_hidden(first, end):
            raw = big.tile([P, (end - first) * HID], BF16, name="hid_raw%d" % first, align_bytes=256, offset=hid_at + first * HID * 2)
            span = span_of(first)
            cols = slice((first - span[0]) * HID, (end - span[0]) * HID)
            nc.sync.dma_start(out=raw[:], in_=rows_of(hidden_states[0, :, :], span)[:, cols])
            for i in range(first, end):
                hid_rows[i] = raw[:, (i - first) * HID : (i - first + 1) * HID]

        def load_a(kp):
            nc.sync.dma_start(out=raw_a[:, kp, :, :].rearrange("p t c -> p (t c)"), in_=wa_dram[kp])

        def load_biases():
            nc.sync.dma_start(out=bias_row[0:1, :], in_=bkva.rearrange("(r c) -> r c", r=1))

        def load_tables(first, end):
            for table, source in ((cos_sb, cos), (sin_sb, sin)):
                nc.sync.dma_start(
                    out=table[:, first:end, :].rearrange("p s d -> p (s d)"),
                    in_=rows_of(source[0, :, :], (first, end)),
                )

        load_a(0)
        load_a(1)
        load_biases()
        load_hidden(0, 2)
        nc.sync.dma_start(out=raw_b[:].rearrange("p t h x -> p (t h x)"), in_=wb_dram)
        load_hidden(2, 4)
        load_tables(0, 8)
        load_hidden(4, 8)
        load_tables(8, 16)
        load_hidden(8, 16)

        ident_f32 = const.tile([P, P], F32)
        make_identity(nc, ident_f32[:])
        biases = const.tile([P, ROPE + PACK], F32)
        rope_bias = biases[:, 0:ROPE]
        lat_bias = biases[:, ROPE:]

        def spread_biases():
            bias_ps = psum_kv.tile([P, ROPE + PACK], F32, name="bias_ps", tag="kv_ps")
            nc.tensor.matmul(out=bias_ps[:, 0:ROPE], lhsT=ones[:], rhs=bias_row[:, RANK:], start=True, stop=True)
            for t in range(PACK):
                nc.tensor.matmul(
                    out=bias_ps[:, ROPE + t : ROPE + t + 1],
                    lhsT=bias_row[:, t:RANK:PACK],
                    rhs=ones[:, 0:1],
                    start=True,
                    stop=True,
                )
            return bias_ps

        a_codes = const.tile([P, HID_PASSES, RANK + ROPE], U32, align_bytes=64)
        a_scales = const.tile([P, HID_PASSES, RANK + ROPE], U8, align_bytes=64)

        grouped_a = {}

        def regroup_a(kp):
            grouped = wstage.tile([P, RANK + ROPE, PACK], BF16, align_bytes=64, name="grouped_a", tag="grouped")
            grouped_a[kp] = grouped
            to = grouped[:, 0:RANK, :].rearrange("p (b m) t -> p b m t", b=PACK)
            source = raw_a[:, kp, :, 0:RANK].rearrange("p t (m b) -> p b m t", b=PACK)
            nc.vector.tensor_copy(out=to[:, 0:2], in_=source[:, 0:2])
            nc.scalar.copy(out=to[:, 2:4], in_=source[:, 2:4])
            nc.vector.tensor_copy(
                out=grouped[:, RANK:, :].rearrange("p (c i) t -> p c t i", i=4),
                in_=raw_a[:, kp, :, RANK:].rearrange("p t (c i) -> p c t i", i=4),
            )

        def quantise_a(kp, cols):
            nc.vector.quantize_mx(
                out=a_codes[:, kp, cols].bitcast(FP8X4),
                scales=a_scales[:, kp, cols],
                in_=grouped_a[kp][:, cols, :].rearrange("p c t -> p (c t)"),
            )

        b_codes = const.tile([P, 3 * KV_CHUNK], U32, align_bytes=64)
        b_scales = const.tile([P, 3 * KV_CHUNK], U8, align_bytes=64)
        b_sources = [
            raw_b[:, :, 0:HALF_HEADS, NOPE:],
            raw_b[:, :, HALF_HEADS:HEADS, NOPE:],
            raw_b[:, :, :, 0:NOPE],
        ]
        grouped_b = {}

        def regroup_b(n, copy, first, end):
            if n not in grouped_b:
                grouped_b[n] = wstage.tile([P, KV_CHUNK, PACK], BF16, align_bytes=64, name="grouped_b", tag="grouped")
            to = grouped_b[n][:].rearrange("p (h d) t -> p h d t", h=b_sources[n].shape[2])
            copy(out=to[:, first:end], in_=b_sources[n][:, :, first:end, :].rearrange("p t h d -> p h d t"))

        def quantise_b(n):
            cols = slice(n * KV_CHUNK, (n + 1) * KV_CHUNK)
            nc.vector.quantize_mx(
                out=b_codes[:, cols].bitcast(FP8X4),
                scales=b_scales[:, cols],
                in_=grouped_b[n][:].rearrange("p c t -> p (c t)"),
            )

        hid_q = {}
        hid_raw = {}
        xts = {}
        kvs = {}
        lat_codes = const.tile([P, TILES, P], U32, align_bytes=64)
        lat_scales = const.tile([P, TILES, P], U8, align_bytes=64)
        lat_ps = {}
        lat_bf = {}
        rope_ps = {}
        rope_sb = {}
        kk_stage = {}
        v_stage = {}

        def run_of(i, runs):
            return [run for run in runs if run[0] <= i < run[1]][0]

        def transpose_hidden(i):
            hid_words = hid_rows[i].bitcast(F32)
            xt = psum_xt.tile([P, HID_PASSES, 2, P], F32, tag="xt")
            for kp in range(HID_PASSES):
                for u in range(2):
                    nc.tensor.transpose(
                        out=xt[:, kp, u, :], in_=hid_words[:, 2 * P * kp + u : 2 * P * (kp + 1) : 2], identity=ident_f32[:]
                    )
            xts[i] = xt

        def empty_transposes(i):
            xt = xts[i]
            hid_raw[i] = work.tile([P, HID_PASSES * P * PACK], BF16, align_bytes=64, name="hid_grouped")
            nc.scalar.copy(
                out=hid_raw[i][:].bitcast(F32).rearrange("p (kp c u) -> p kp c u", kp=HID_PASSES, u=2),
                in_=xt[:].rearrange("p kp u c -> p kp c u"),
            )

        def quantise_hidden(i):
            hid_codes = work.tile([P, HID_PASSES, P], U32, align_bytes=64)
            hid_scales = work.tile([P, HID_PASSES, P], U8, align_bytes=64)
            nc.vector.quantize_mx(
                out=hid_codes[:].rearrange("p kp c -> p (kp c)").bitcast(FP8X4),
                scales=hid_scales[:].rearrange("p kp c -> p (kp c)"),
                in_=hid_raw[i][:],
            )
            hid_q[i] = (hid_codes, hid_scales)

        def first_matmul(i):
            r, j = divmod(i, PAIR)
            hid_codes, hid_scales = hid_q[i]
            lat_ps[i] = psum_lat.tile([P, PACK, P], F32, name="lat_ps")
            for t in range(PACK):
                for kp in range(HID_PASSES):
                    nc.tensor.matmul_mx(
                        out=lat_ps[i][:, t, :],
                        lhsT=a_codes[:, kp, t * P : (t + 1) * P].bitcast(FP8X4),
                        lhsT_scale=a_scales[:, kp, t * P : (t + 1) * P],
                        rhs=hid_codes[:, kp, :].bitcast(FP8X4),
                        rhs_scale=hid_scales[:, kp, :],
                        start=(kp == 0),
                        stop=(kp == HID_PASSES - 1),
                    )
            if j == 0:
                rope_ps[r] = psum_rope.tile([P, PAIR, ROPE], F32, name="rope_ps")
            for kp in range(HID_PASSES):
                nc.tensor.matmul_mx(
                    out=rope_ps[r][:, j, :],
                    lhsT=hid_codes[:, kp, :].bitcast(FP8X4),
                    lhsT_scale=hid_scales[:, kp, :],
                    rhs=a_codes[:, kp, RANK : RANK + ROPE].bitcast(FP8X4),
                    rhs_scale=a_scales[:, kp, RANK : RANK + ROPE],
                    start=(kp == 0),
                    stop=(kp == HID_PASSES - 1),
                )

        def add_latent_bias(i):
            lat_bf[i] = work.tile([P, P, PACK], BF16, align_bytes=64, name="lat_grouped")
            nc.vector.tensor_tensor(
                out=lat_bf[i][:],
                in0=lat_ps[i][:].rearrange("p t c -> p c t"),
                in1=lat_bias.unsqueeze(1).to_broadcast([P, P, PACK]),
                op=ADD,
            )

        def quantise_latents(i):
            nc.vector.quantize_mx(
                out=lat_codes[:, i, :].bitcast(FP8X4),
                scales=lat_scales[:, i, :],
                in_=lat_bf[i][:].rearrange("p c t -> p (c t)"),
            )

        def kk_tile(i):
            first, end = run_of(i, K_RUNS)
            if first not in kk_stage:
                kk_stage[first] = big.tile(
                    [P, HEADS, end - first, KDIM], F32, name="kk_stage%d" % first, align_bytes=256, offset=kk_at[first]
                )
            return kk_stage[first], i - first

        def rotate(r, part):
            if part == 0:
                rope_sb[r] = (
                    rope_pool.tile([P, PAIR, ROPE], F32, name="k_rope"),
                    rope_pool.tile([P, PAIR, ROPE], F32, name="k_rot"),
                    rope_pool.tile([P, PAIR, ROPE], F32, name="crossed"),
                )
            k_rope, k_rot, crossed = rope_sb[r]
            tiles = slice(r * PAIR, (r + 1) * PAIR)
            lo = slice(0, HALF_ROPE)
            hi = slice(HALF_ROPE, ROPE)
            if part == 0:
                nc.vector.tensor_tensor(
                    out=k_rope[:],
                    in0=rope_ps[r][:],
                    in1=rope_bias.unsqueeze(1).to_broadcast([P, PAIR, ROPE]),
                    op=ADD,
                )
            if part == 1:
                nc.vector.tensor_tensor(out=k_rot[:], in0=k_rope[:], in1=cos_sb[:, tiles, :], op=MULT)
                nc.vector.scalar_tensor_tensor(
                    out=crossed[:, :, lo], in0=k_rope[:, :, hi], scalar=-1.0, in1=sin_sb[:, tiles, lo], op0=MULT, op1=MULT
                )
                nc.vector.tensor_tensor(out=crossed[:, :, hi], in0=k_rope[:, :, lo], in1=sin_sb[:, tiles, hi], op=MULT)
            if part == 2:
                stage, j = kk_tile(r * PAIR)
                nc.vector.tensor_tensor(out=stage[:, 0, j : j + PAIR, NOPE:], in0=k_rot[:], in1=crossed[:], op=ADD)
            if part >= 3:
                stage, j = kk_tile(r * PAIR)
                heads = slice(1, HALF_HEADS) if part == 3 else slice(HALF_HEADS, HEADS)
                nc.vector.tensor_copy(
                    out=stage[:, heads, j : j + PAIR, NOPE:],
                    in_=stage[:, 0, j : j + PAIR, NOPE:]
                    .unsqueeze(1)
                    .to_broadcast([P, heads.stop - heads.start, PAIR, ROPE]),
                )

        def second(i, n):
            kv_ps = psum_kv.tile([P, KV_CHUNK], F32, name="kv_ps", tag="kv_ps")
            cols = slice(n * KV_CHUNK, (n + 1) * KV_CHUNK)
            nc.tensor.matmul_mx(
                out=kv_ps[:],
                lhsT=lat_codes[:, i, :].bitcast(FP8X4),
                lhsT_scale=lat_scales[:, i, :],
                rhs=b_codes[:, cols].bitcast(FP8X4),
                rhs_scale=b_scales[:, cols],
                start=True,
                stop=True,
            )
            kvs[(i, n)] = kv_ps

        def empty_second(i, n, copy):
            kv_ps = kvs[(i, n)]
            if n == K_CHUNK:
                stage, j = kk_tile(i)
                copy(out=stage[:, :, j, 0:NOPE], in_=kv_ps[:].rearrange("p (h d) -> p h d", d=NOPE))
            else:
                first, end = run_of(i, V_RUNS)
                if first not in v_stage:
                    v_stage[first] = big.tile(
                        [P, HEADS, end - first, VDIM], F32, name="v_stage%d" % first, align_bytes=256, offset=v_at[first]
                    )
                heads = slice(n * HALF_HEADS, (n + 1) * HALF_HEADS)
                copy(out=v_stage[first][:, heads, i - first, :], in_=kv_ps[:].rearrange("p (h d) -> p h d", d=VDIM))

        def store(dram, stage, run, d, heads, pieces=1):
            first, end = run
            span = span_of(first)
            at = (first - span[0]) * d
            whole = (end - first) * d
            cuts = (0, whole) if pieces == 1 else (0, whole * 2 // 3, whole)
            for lo, hi in zip(cuts, cuts[1:]):
                nc.sync.dma_start(
                    out=head_rows_of(dram[0, :, :, :], span)[:, heads, at + lo : at + hi],
                    in_=stage[first][:, heads, :, :].rearrange("p h j d -> p h (j d)")[:, :, lo:hi],
                )

        HALVES = (slice(0, HALF_HEADS), slice(HALF_HEADS, HEADS))
        ALL = slice(0, HEADS)

        vector_copy = nc.vector.tensor_copy
        scalar_copy = nc.scalar.copy
        LATENT = slice(0, RANK)
        ROPES = slice(RANK, RANK + ROPE)

        with tc.manual_schedule():
            def unit(i, n):
                second(i, n)
                empty_second(i, n, scalar_copy)

            for k in range(14):
                warm_ps = psum_kv.tile([P, KV_CHUNK], F32, name="warm_ps", tag="kv_ps")
                nc.tensor.matmul(out=warm_ps[:], lhsT=ones[:], rhs=blank[:], start=True, stop=True)
            transpose_hidden(0)
            transpose_hidden(1)
            bias_ps = spread_biases()
            for k in range(3):
                warm_ps = psum_kv.tile([P, KV_CHUNK], F32, name="warm_ps", tag="kv_ps")
                nc.tensor.matmul(out=warm_ps[:], lhsT=ones[:], rhs=blank[:], start=True, stop=True)
            regroup_a(0)
            quantise_a(0, LATENT)
            regroup_a(1)
            quantise_a(1, LATENT)
            empty_transposes(0)
            empty_transposes(1)
            quantise_hidden(0)
            quantise_a(0, ROPES)
            quantise_a(1, ROPES)
            quantise_hidden(1)
            nc.vector.tensor_copy(out=biases[:], in_=bias_ps[:])
            first_matmul(0)
            first_matmul(1)
            transpose_hidden(2)
            transpose_hidden(3)
            add_latent_bias(0)
            regroup_b(0, vector_copy, 0, 2)
            regroup_b(0, scalar_copy, 2, 4)
            regroup_b(2, scalar_copy, 6, 8)
            empty_transposes(2)
            empty_transposes(3)
            regroup_b(1, scalar_copy, 2, 4)
            add_latent_bias(1)
            quantise_b(0)
            quantise_latents(0)
            quantise_latents(1)
            rotate(0, 0)
            quantise_hidden(2)
            regroup_b(1, vector_copy, 0, 2)
            quantise_hidden(3)
            unit(0, 0)
            unit(1, 0)
            first_matmul(2)
            first_matmul(3)
            quantise_b(1)
            add_latent_bias(2)
            add_latent_bias(3)
            rotate(1, 0)
            quantise_latents(2)
            quantise_latents(3)
            regroup_b(2, vector_copy, 0, 6)
            store(out_1, v_stage, (0, 2), VDIM, HALVES[0])
            unit(0, 1)
            unit(1, 1)
            store(out_1, v_stage, (0, 2), VDIM, HALVES[1])
            transpose_hidden(4)
            empty_transposes(4)
            quantise_hidden(4)
            quantise_b(K_CHUNK)
            for i in (2, 3):
                unit(i, 0)
            store(out_1, v_stage, (2, 4), VDIM, HALVES[0])
            transpose_hidden(5)
            empty_transposes(5)
            for i in (2, 3):
                unit(i, 1)
            store(out_1, v_stage, (2, 4), VDIM, HALVES[1])
            first_matmul(4)
            unit(0, 2)
            unit(1, 2)
            transpose_hidden(6)
            empty_transposes(6)
            unit(2, 2)
            unit(3, 2)
            rotate(0, 1)
            rotate(1, 1)
            rotate(0, 2)
            quantise_hidden(5)
            rotate(0, 3)
            store(out_0, kk_stage, (0, 2), KDIM, HALVES[0])
            rotate(0, 4)
            store(out_0, kk_stage, (0, 2), KDIM, HALVES[1])
            add_latent_bias(4)
            rotate(1, 2)
            quantise_latents(4)
            rotate(1, 3)
            rotate(1, 4)
            store(out_0, kk_stage, (2, 4), KDIM, ALL, 2)
            for s in range(5, TILES + 2):
                r, late = divmod(s - PAIR, PAIR)
                units = [(s - 1, 0), (s - 1, 1)] if s <= TILES else []
                if s > 5:
                    units.append((s - 2, K_CHUNK))
                if s < TILES:
                    first_matmul(s)
                ahead = 0 if s == 5 else 1
                for i, n in units[:ahead]:
                    unit(i, n)
                if s % 2 == 1:
                    for i in range(s + 2, min(s + 4, TILES)):
                        transpose_hidden(i)
                if s + 2 < TILES:
                    empty_transposes(s + 2)
                for i, n in units[ahead:]:
                    unit(i, n)
                if s + 1 < TILES:
                    quantise_hidden(s + 1)
                if r < PAIRS and s > 5:
                    rotate(r, 3 if late else 1)
                if s < TILES:
                    add_latent_bias(s)
                if late and s < TILES:
                    rotate(r + 1, 0)
                if r < PAIRS and s > 5:
                    rotate(r, 4 if late else 2)
                if s < TILES:
                    quantise_latents(s)
                for run in V_RUNS[2:]:
                    if s == run[1]:
                        store(out_1, v_stage, run, VDIM, ALL)
                for run in K_RUNS[2:]:
                    if s == run[1] + 1:
                        store(out_0, kk_stage, run, KDIM, ALL, 2)
